import numpy as np
import ml_dtypes


def mxq(x, axis, fmt="e4m3"):
    dtype, down = {"e4m3": (ml_dtypes.float8_e4m3fn, 7), "e5m2": (ml_dtypes.float8_e5m2, 14)}[fmt]
    v = np.moveaxis(np.asarray(x, np.float32).astype(ml_dtypes.bfloat16).astype(np.float64), axis, -1)
    blocks = v.reshape(v.shape[:-1] + (-1, 32))
    amax = np.abs(blocks).max(-1, keepdims=True)
    byte = np.maximum(np.where(amax > 0, np.frexp(amax)[1] - 1 + 127, 0) - down, 1)
    scale = np.exp2(byte - 127.0)
    codes = (blocks / scale).astype(np.float32).astype(dtype).astype(np.float64)
    return np.moveaxis((codes * scale).reshape(v.shape), -1, axis)


WIDE = False


def mx_kscale(k):
    if not WIDE:
        return np.ones(k)
    levels = np.array([10, -10, 5, -5, 0])
    if k % 512:
        return np.exp2(np.random.permutation(np.resize(levels, k // 32))).repeat(32)
    a = np.empty((k // 512, 16))
    for p in range(k // 512):
        a[p, :8] = np.random.permutation(np.resize(levels, 8))
        for g in range(8):
            far = levels[np.abs(levels - a[p, g]) >= 10]
            a[p, g + 8] = far[np.random.randint(len(far))]
    return np.exp2(a.ravel()).repeat(32)


BF16 = ml_dtypes.bfloat16


def bf(x):
    return np.asarray(x, np.float32).astype(BF16)


def f64(x):
    return np.asarray(x).astype(np.float64)


E2M1 = np.array([0.0, 0.5, 1.0, 1.5, 2.0, 3.0, 4.0, 6.0, -0.0, -0.5, -1.0, -1.5, -2.0, -3.0, -4.0, -6.0])


def pack_weight(w, fmt):
    k, n = w.shape
    w = f64(bf(w)).reshape(k // 32, 32, n)
    amax = np.abs(w).max(1)
    if fmt == "e4m3":
        byte = np.frexp(amax)[1] - 1 + 127 - 7
    else:
        mant, ex = np.frexp(amax / 6.0)
        byte = np.where(mant > 0.5, ex, ex - 1) + 127
    byte = np.clip(np.where(amax > 0, byte, 1), 1, 254)
    scaled = (w * np.exp2(127.0 - byte)[:, None, :]).reshape(k, n).astype(np.float32)
    by_word = np.ascontiguousarray(scaled.reshape(k // 512, 128, 4, n).transpose(0, 1, 3, 2))
    if fmt == "e4m3":
        words = by_word.astype(ml_dtypes.float8_e4m3fn).view(np.uint8)
    else:
        c = by_word.astype(ml_dtypes.float4_e2m1fn).view(np.uint8) & 0xF
        words = c[..., 0::2] | (c[..., 1::2] << 4)
    return np.ascontiguousarray(words), np.ascontiguousarray(byte.astype(np.uint8).reshape(k // 512, 16, n))


def unpack_weight(words, scales, fmt):
    g, p, n, _ = words.shape
    if fmt == "e4m3":
        vals = np.ascontiguousarray(words).view(ml_dtypes.float8_e4m3fn).astype(np.float64)
    else:
        nib = np.empty((g, p, n, 4), np.uint8)
        nib[..., 0::2] = words & 0xF
        nib[..., 1::2] = words >> 4
        vals = E2M1[nib]
    vals = vals * np.repeat(np.exp2(scales.astype(np.float64) - 127.0), 8, axis=1)[..., None]
    return vals.transpose(0, 1, 3, 2).reshape(g * 512, n)
def pack4(w):
    words, scales = pack_weight(w, "e2m1")
    return words.reshape(words.shape[0], 128, -1), scales


def unpack4(words, scales):
    return unpack_weight(words.reshape(words.shape[0], 128, -1, 2), scales, "e2m1")


B, N, F, K = 16, 512, 512, 256
BN_EPS = 1e-5
NORM_EPS = 1e-12


def draw0():
    s, t = mx_kscale(N), mx_kscale(F)
    deg = np.random.uniform(0.5, 1.5, size=(B, N, 1))
    x = bf(np.random.standard_normal((B, N, F)) * 0.5 / s[:, None] * t)
    adj = bf(np.random.uniform(size=(B, N, N)) * deg * 4.0 / np.sqrt(N) * s)
    words, scales = pack4(np.random.standard_normal((F, K)) / np.sqrt(F) / t[:, None])
    return {"x": x,
            "adj": adj,
            "W_words": words,
            "W_scales": scales,
            "b": bf(np.random.standard_normal(K) * 0.2)}


def core(x, adj, W_words, W_scales, b):
    agg = mxq(f64(adj), 2, "e4m3") @ mxq(f64(x), 1, "e4m3")
    h = (mxq(agg, 2, "e4m3") @ unpack4(W_words, W_scales)) + f64(b)
    nrm = np.sqrt(np.sum(h * h, axis=2, keepdims=True))
    h = h / np.maximum(nrm, NORM_EPS)
    h = np.maximum(h, 0.0)
    mean = np.mean(h, axis=(0, 2), keepdims=True)
    var = np.var(h, axis=(0, 2), keepdims=True)
    return (h - mean) / np.sqrt(var + BN_EPS)


def e4m3fn_bytes(y):
    return np.clip(np.asarray(y, np.float64), -448.0, 448.0).astype(np.float32).astype(ml_dtypes.float8_e4m3fn).view(np.uint8)


def e4m3fn_values(b):
    return np.asarray(b, np.uint8).view(ml_dtypes.float8_e4m3fn).astype(np.float64)


def setup_inputs():
    d = draw0()
    x0 = np.asarray(d['adj']).astype(np.float64)
    s = (np.max(np.abs(x0), axis=(0, 1), keepdims=True) / 448.0).astype(np.float32)
    out = {}
    for k, v in d.items():
        if k == 'adj':
            out['adj_bytes'] = e4m3fn_bytes(x0 / s.astype(np.float64))
            out['adj_scale'] = s
        else:
            out[k] = v
    return out


def reference(x, adj_bytes, adj_scale, W_words, W_scales, b):
    return core(x, e4m3fn_values(adj_bytes) * adj_scale.astype(np.float64), W_words, W_scales, b)

@@ -1,0 +1,333 @@
+from contextlib import ExitStack
+
+import concourse.mybir as mybir
+from concourse.masks import make_identity
+
+G, N, F, K = 16, 512, 512, 256
+P = 128
+FLOPS = 2 * G * N * N * F + 2 * G * N * F * K
+BN_EPS = 1e-5
+NORM_EPS = 1e-12
+
+F32 = mybir.dt.float32
+BF16 = mybir.dt.bfloat16
+U32 = mybir.dt.uint32
+I32 = mybir.dt.int32
+U8 = mybir.dt.uint8
+FP8 = mybir.dt.float8_e4m3fn
+FP8X4 = mybir.dt.float8_e4m3fn_x4
+FP4X4 = mybir.dt.float4_e2m1fn_x4
+ACT = mybir.ActivationFunctionType
+ALU = mybir.AluOpType
+AXX = mybir.AxisListType.X
+
+STEPS = 32
+PH1, PH2 = 16, 24
+
+
+def tile_routingassignment_pa_t_w4_kernel(tc, x, adj_bytes, adj_scale, W_words, W_scales, b, out):
+    nc = tc.nc
+    with ExitStack() as ctx:
+        keep = ctx.enter_context(tc.tile_pool(name="keep", bufs=1))
+        stream = ctx.enter_context(tc.tile_pool(name="stream", bufs=3))
+        psum = ctx.enter_context(tc.psum_pool(name="psum", bufs=2))
+
+        warm = keep.tile([P, 1], F32, name="warm")
+        warm2 = keep.tile([P, 1], F32, name="warm2")
+        nc.vector.memset(warm[:], 1.0)
+        nc.scalar.activation(out=warm2[:], in_=warm[:], func=ACT.Sqrt)
+
+        scale_col = keep.tile([P, 4], F32, name="scale_col")
+        with nc.allow_non_contiguous_dma(reason="one scale to a partition"):
+            nc.scalar.dma_start(out=scale_col[:], in_=adj_scale.rearrange("a b (m q) -> q (a b m)", q=P))
+
+        x_raw = {}
+
+        def load_x(g):
+            x_raw[g] = stream.tile([P, 4, F], BF16, name="x_raw", bufs=6)
+            nc.sync.dma_start(out=x_raw[g][:], in_=x[g].rearrange("(p t) f -> p t f", t=4))
+
+        adj1 = {}
+
+        def load_adj1(c, g0, g1):
+            t = keep.tile([P, g1 - g0, 2 * N], U8, name="adj1_%d" % c)
+            nc.sync.dma_start(out=t[:], in_=adj_bytes[g0:g1, 0:256, :].rearrange("g (p r) j -> p g (r j)", r=2))
+            for g in range(g0, g1):
+                adj1[g] = (t, g - g0)
+
+        load_x(0)
+        load_adj1(0, 0, 2)
+        load_x(1)
+        load_adj1(1, 2, 4)
+        load_x(2)
+        w_sb = keep.tile([P, 2 * K], U8, name="w_sb", align_bytes=64)
+        nc.sync.dma_start(out=w_sb[:], in_=W_words[0])
+        w_sc = keep.tile([P, K], U8, name="w_sc", align_bytes=64)
+        ident = keep.tile([P, P], F32, name="ident")
+        make_identity(nc, ident[:])
+        nc.gpsimd.memset(w_sc[:].bitcast(U32), 0)
+        for q in range(4):
+            nc.sync.dma_start(out=w_sc[32 * q : 32 * q + 4, :].bitcast(I32), in_=W_scales[0, 4 * q : 4 * q + 4, :].bitcast(I32))
+        b_row = keep.tile([P, K], BF16, name="b_row")
+        nc.gpsimd.memset(b_row[:], 0.0)
+        ones = keep.tile([P, P], BF16, name="ones")
+        nc.gpsimd.memset(ones[:], 1.0)
+        nc.scalar.dma_start(out=b_row[0:1, :], in_=b.rearrange("(o c) -> o c", o=1))
+        load_x(3)
+        load_adj1(2, 4, 8)
+        load_x(4)
+        load_x(5)
+
+        scale2 = keep.tile([P, 2, N], F32, name="scale2")
+        bias2 = keep.tile([P, 2, K], F32, name="bias2")
+
+        xc = [keep.tile([P, F], U32, name="xc%d" % g, align_bytes=64) for g in range(G)]
+        xs = [keep.tile([P, F], U8, name="xs%d" % g, align_bytes=64) for g in range(G)]
+        r1 = keep.tile([P, G, 2, K], F32, name="r1")
+        r2 = keep.tile([P, G, K], F32, name="r2")
+        r3 = keep.tile([P, G, K], F32, name="r3")
+        sum1 = keep.tile([P, G, 2], F32, name="sum1")
+        sq1 = keep.tile([P, 2, 8], F32, name="sq1")
+        bst = {2: keep.tile([P, 8, 6], F32, name="bst2"), 3: keep.tile([P, 8, 6], F32, name="bst3")}
+        adj2 = keep.tile([P, G, N], U8, name="adj2")
+        adj3 = keep.tile([P, G, N], U8, name="adj3")
+
+        x_grp, sc, psT, ag, ac, asc, psA, gg, gc, gsc, psH, h, ss, rinv = ({} for _ in range(14))
+
+        def graphs(s):
+            return (s, s) if s < PH1 else (2 * ((s - PH1) % 8), 2 * ((s - PH1) % 8) + 1)
+
+        def x_group(g, half):
+            if half == 0:
+                x_grp[g] = stream.tile([P, 4, P, 4], BF16, name="x_grp", bufs=2, align_bytes=64)
+            c = slice(2 * half, 2 * half + 2)
+            nc.vector.tensor_copy(out=x_grp[g][:, c], in_=x_raw[g][:].rearrange("p t (m c) -> p c m t", c=4)[:, c])
+
+        def x_quant(g):
+            nc.vector.quantize_mx(out=xc[g][:].bitcast(FP8X4), scales=xs[g][:], in_=x_grp[g][:].rearrange("p c m t -> p (c m t)"))
+
+        def adj_scale_mul(s):
+            sc[s] = stream.tile([P, 2 * N], BF16, name="sc", align_bytes=64)
+            if s < PH1:
+                t, i = adj1[s]
+                src = t[:, i, :]
+            else:
+                g0, g1 = graphs(s)
+                src = (adj2 if s < PH2 else adj3)[:, g0 : g1 + 1, :].rearrange("p g j -> p (g j)")
+            nc.vector.tensor_tensor(out=sc[s][:], in0=src.bitcast(FP8), in1=scale2[:].rearrange("p a j -> p (a j)"), op=ALU.mult)
+
+        def adj_transpose(s):
+            psT[s] = psum.tile([P, 2, 2, P], F32, name="psT", bufs=2)
+            words = sc[s][:].bitcast(F32)
+            for a in range(2):
+                for u in range(2):
+                    nc.tensor.transpose(psT[s][:, a, u, :], words[:, 256 * a + u : 256 * (a + 1) : 2], ident[:])
+
+        def adj_exit(s):
+            ag[s] = stream.tile([P, 8 * P], BF16, name="ag", align_bytes=64)
+            nc.scalar.copy(out=ag[s][:].bitcast(F32).rearrange("p (a n u) -> p a n u", a=2, u=2), in_=psT[s][:].rearrange("p a u n -> p a n u"))
+
+        def adj_quant(s):
+            ac[s] = stream.tile([P, 2 * P], U32, name="ac", align_bytes=64)
+            asc[s] = stream.tile([P, 2 * P], U8, name="asc", align_bytes=64)
+            nc.vector.quantize_mx(out=ac[s][:].bitcast(FP8X4), scales=asc[s][:], in_=ag[s][:])
+
+        def agg_matmul(s):
+            gr = graphs(s)
+            for a in range(2):
+                psA[s, a] = psum.tile([P, 4, P], F32, name="psA", bufs=4)
+                rows = slice(P * a, P * (a + 1))
+                for t in range(4):
+                    cols = slice(P * t, P * (t + 1))
+                    nc.tensor.matmul_mx(
+                        out=psA[s, a][:, t, :],
+                        lhsT=xc[gr[a]][:, cols].bitcast(FP8X4), lhsT_scale=xs[gr[a]][:, cols],
+                        rhs=ac[s][:, rows].bitcast(FP8X4), rhs_scale=asc[s][:, rows],
+                        start=True, stop=True)
+
+        def agg_exit(s):
+            gg[s] = stream.tile([P, 2, P, 4], BF16, name="gg", align_bytes=64)
+            for a in range(2):
+                nc.scalar.copy(out=gg[s][:, a], in_=psA[s, a][:].rearrange("p t n -> p n t"))
+
+        def agg_quant(s):
+            gc[s] = stream.tile([P, 2 * P], U32, name="gc", align_bytes=64)
+            gsc[s] = stream.tile([P, 2 * P], U8, name="gsc", align_bytes=64)
+            nc.vector.quantize_mx(out=gc[s][:].bitcast(FP8X4), scales=gsc[s][:], in_=gg[s][:].rearrange("p a n t -> p (a n t)"))
+
+        def h_matmul(s):
+            psH[s] = psum.tile([P, 2, K], F32, name="psH", bufs=2)
+            for a in range(2):
+                rows = slice(P * a, P * (a + 1))
+                nc.tensor.matmul_mx(
+                    out=psH[s][:, a, :],
+                    lhsT=gc[s][:, rows].bitcast(FP8X4), lhsT_scale=gsc[s][:, rows],
+                    rhs=w_sb[:].bitcast(FP4X4), rhs_scale=w_sc[:],
+                    start=True, stop=True)
+
+        def h_bias(s):
+            h[s] = stream.tile([P, 2, K], F32, name="h", bufs=5)
+            nc.vector.tensor_tensor(out=h[s][:], in0=psH[s][:], in1=bias2[:], op=ALU.add)
+
+        def h_square(s):
+            if s % 2 == 0:
+                ss[s // 2] = stream.tile([P, 4], F32, name="ss")
+            for a in range(2):
+                junk = stream.tile([P, K], F32, name="junk", bufs=2)
+                col = 2 * (s % 2) + a
+                nc.scalar.activation(out=junk[:], in_=h[s][:, a, :], func=ACT.Square, accum_out=ss[s // 2][:, col : col + 1])
+
+        def norm_root(m):
+            ssm = stream.tile([P, 4], F32, name="ssm")
+            nc.gpsimd.tensor_scalar(out=ssm[:], in0=ss[m][:], scalar1=NORM_EPS * NORM_EPS, scalar2=None, op0=ALU.max)
+            rinv[m] = stream.tile([P, 4], F32, name="rinv")
+            nrm = stream.tile([P, 4], F32, name="nrm")
+            nc.scalar.activation(out=nrm[:], in_=ssm[:], func=ACT.Sqrt)
+            ss[m] = nrm
+
+        def norm_recip(m):
+            nc.vector.reciprocal(out=rinv[m][:], in_=ss[m][:])
+
+        def relu(s):
+            g0, g1 = graphs(s)
+            for a in range(2):
+                sc_ap = rinv[s // 2][:, 2 * (s % 2) + a : 2 * (s % 2) + a + 1]
+                if s < PH1:
+                    nc.scalar.activation(out=r1[:, g0, a, :], in_=h[s][:, a, :], func=ACT.Relu, scale=sc_ap, accum_out=sum1[:, g0, a : a + 1])
+                else:
+                    dst = r2 if s < PH2 else r3
+                    nc.scalar.activation(out=dst[:, g0 + a, :], in_=h[s][:, a, :], func=ACT.Relu, scale=sc_ap)
+
+        def sq_sum1(j, a):
+            junk2 = stream.tile([P, 2, K], F32, name="junk2", bufs=2)
+            nc.scalar.activation(out=junk2[:], in_=r1[:, 2 * j : 2 * j + 2, a, :], func=ACT.Square, accum_out=sq1[:, a, j : j + 1])
+
+        def stats23(s):
+            g0, g1 = graphs(s)
+            src = r2 if s < PH2 else r3
+            i = (s - PH1) % 8
+            nc.vector.bn_stats(out=bst[2 if s < PH2 else 3][:, i, :], in_=src[:, g0 : g1 + 1, :].rearrange("p g c -> p (g c)"))
+
+        mean, root, coef = {}, {}, {}
+
+        def finish_a(ph):
+            n = 2 if ph == 1 else 1
+            varp = keep.tile([P, n], F32, name="varp%d" % ph)
+            if ph == 1:
+                mean[1] = keep.tile([P, 2], F32, name="mean1")
+                e2 = keep.tile([P, 2], F32, name="e2")
+                m2 = keep.tile([P, 2], F32, name="m2")
+                nc.vector.tensor_reduce(out=mean[1][:], in_=sum1[:].rearrange("p g a -> p a g"), axis=AXX, op=ALU.add)
+                nc.vector.tensor_reduce(out=e2[:], in_=sq1[:], axis=AXX, op=ALU.add)
+                nc.vector.tensor_scalar(out=mean[1][:], in0=mean[1][:], scalar1=1.0 / (G * K), scalar2=None, op0=ALU.mult)
+                nc.vector.tensor_tensor(out=m2[:], in0=mean[1][:], in1=mean[1][:], op=ALU.mult)
+                nc.vector.scalar_tensor_tensor(out=varp[:], in0=e2[:], scalar=1.0 / (G * K), in1=m2[:], op0=ALU.mult, op1=ALU.subtract)
+                nc.vector.tensor_scalar(out=varp[:], in0=varp[:], scalar1=BN_EPS, scalar2=None, op0=ALU.add)
+            else:
+                mv = keep.tile([P, 2], F32, name="mv%d" % ph)
+                nc.vector.bn_aggr(out=mv[:], in_=bst[ph][:].rearrange("p i s -> p (i s)"))
+                mean[ph] = mv
+                nc.vector.tensor_scalar(out=varp[:], in0=mv[:, 1:2], scalar1=BN_EPS, scalar2=None, op0=ALU.add)
+            root[ph] = keep.tile([P, n], F32, name="root%d" % ph)
+            nc.scalar.activation(out=root[ph][:], in_=varp[:], func=ACT.Sqrt)
+
+        def finish_b(ph):
+            n = 2 if ph == 1 else 1
+            a = keep.tile([P, n], F32, name="a%d" % ph)
+            c = keep.tile([P, n], F32, name="c%d" % ph)
+            nc.vector.reciprocal(out=a[:], in_=root[ph][:])
+            nc.vector.scalar_tensor_tensor(out=c[:], in0=mean[ph][:, 0:n], scalar=-1.0, in1=a[:], op0=ALU.mult, op1=ALU.mult)
+            coef[ph] = (a, c)
+
+        def emit(ph, q, i):
+            a, c = coef[ph]
+            g4 = slice(4 * q, 4 * q + 4)
+            t = r1[:, g4, i, :] if ph == 1 else (r2 if ph == 2 else r3)[:, g4, :]
+            nc.vector.tensor_scalar(out=t, in0=t, scalar1=a[:, i : i + 1], scalar2=c[:, i : i + 1], op0=ALU.mult, op1=ALU.add)
+            if ph == 1 and i == 1:
+                nc.sync.dma_start(out=out[g4, 0:256, :].rearrange("g (p r) c -> p g (r c)", r=2), in_=r1[:, g4].rearrange("p g r c -> p g (r c)"))
+            if ph > 1:
+                n0 = 256 if ph == 2 else 384
+                nc.sync.dma_start(out=out[g4, n0 : n0 + P, :].rearrange("g p c -> p g c"), in_=t)
+
+        todo = []
+
+        with tc.manual_schedule():
+            psc = psum.tile([P, 4, P], F32, name="psA", bufs=4)
+            for m in range(4):
+                nc.tensor.transpose(psc[:, m, :], scale_col[:, m : m + 1].to_broadcast([P, P]), ident[:])
+            x_group(0, 0)
+            x_group(0, 1)
+            nc.scalar.copy(out=scale2[:, 0, :], in_=psc[:].rearrange("p m q -> p (m q)"))
+            nc.scalar.copy(out=scale2[:, 1, :], in_=psc[:].rearrange("p m q -> p (m q)"))
+            adj_scale_mul(0)
+            x_quant(0)
+            psb = psum.tile([P, 2, K], F32, name="psH", bufs=2)
+            for a in range(2):
+                nc.tensor.matmul(psb[:, a, :], lhsT=ones[:], rhs=b_row[:], start=True, stop=True)
+            nc.scalar.copy(out=bias2[:], in_=psb[:])
+
+            for k in range(STEPS + 8):
+                if k + 6 < G:
+                    load_x(k + 6)
+                if k == 1:
+                    load_adj1(3, 8, 16)
+                if k == 9:
+                    nc.sync.dma_start(out=adj2[:], in_=adj_bytes[:, 256:384, :].rearrange("g p j -> p g j"))
+                    nc.sync.dma_start(out=adj3[:], in_=adj_bytes[:, 384:512, :].rearrange("g p j -> p g j"))
+                if k < STEPS:
+                    adj_transpose(k)
+                if 0 <= k - 1 < STEPS:
+                    adj_quant(k - 1)
+                if 0 <= k - 2 < STEPS:
+                    agg_quant(k - 2)
+                if 0 <= k - 1 < STEPS:
+                    agg_matmul(k - 1)
+                if 0 <= k - 2 < STEPS:
+                    h_matmul(k - 2)
+                if k % 2 == 1 and 0 <= k - 5 < STEPS:
+                    norm_recip((k - 5) // 2)
+                if k + 1 < G:
+                    x_group(k + 1, 0)
+                if k + 1 < STEPS:
+                    adj_scale_mul(k + 1)
+                if k + 1 < G:
+                    x_group(k + 1, 1)
+                if 0 <= k - 2 < STEPS:
+                    h_bias(k - 2)
+                if k + 1 < G:
+                    x_quant(k + 1)
+                if 0 <= k - 3 < STEPS:
+                    h_square(k - 3)
+                if k < STEPS:
+                    adj_exit(k)
+                if 0 <= k - 1 < STEPS:
+                    agg_exit(k - 1)
+                if k % 2 == 0 and 0 <= k - 4 < STEPS:
+                    norm_root((k - 4) // 2)
+                if 0 <= k - 5 < STEPS:
+                    relu(k - 5)
+                if k % 2 == 0 and 0 <= k - 6 < PH1:
+                    sq_sum1((k - 6) // 2, 0)
+                if k % 2 == 1 and 0 <= k - 7 < PH1:
+                    sq_sum1((k - 7) // 2, 1)
+                if PH1 <= k - 6 < STEPS:
+                    stats23(k - 6)
+                if todo:
+                    emit(*todo.pop(0))
+                if k == PH1 + 6:
+                    finish_a(1)
+                if k == PH1 + 7:
+                    finish_b(1)
+                    todo += [(1, q, i) for q in range(4) for i in range(2)]
+                if k == PH2 + 5:
+                    finish_a(2)
+                if k == PH2 + 6:
+                    finish_b(2)
+                    todo += [(2, q, 0) for q in range(4)]
+            finish_a(3)
+            for e in todo:
+                emit(*e)
+            finish_b(3)
+            for q in range(4):
+                emit(3, q, 0)

@@ -100,8 +100,8 @@ def tile_routingassignment_pa_t_w4_kernel(tc, x, adj_bytes, adj_scale, W_words, 
         def x_group(g, half):
             if half == 0:
                 x_grp[g] = stream.tile([P, 4, P, 4], BF16, name="x_grp", bufs=2, align_bytes=64)
-            c = slice(2 * half, 2 * half + 2)
-            nc.vector.tensor_copy(out=x_grp[g][:, c], in_=x_raw[g][:].rearrange("p t (m c) -> p c m t", c=4)[:, c])
+            m = slice(64 * half, 64 * half + 64)
+            nc.vector.tensor_copy(out=x_grp[g][:].rearrange("p c m t -> p m c t")[:, m], in_=x_raw[g][:].rearrange("p t (m c) -> p m c t", c=4)[:, m])
 
         def x_quant(g):
             nc.vector.quantize_mx(out=xc[g][:].bitcast(FP8X4), scales=xs[g][:], in_=x_grp[g][:].rearrange("p c m t -> p (c m t)"))

@@ -21,12 +21,80 @@ ACT = mybir.ActivationFunctionType
 ALU = mybir.AluOpType
 AXX = mybir.AxisListType.X
 
-STEPS = 32
-PH1, PH2 = 16, 24
+MIX = 1
+BN = (2, 3)
+XPARTS = 4
+XS = 1
+EXV = 0
+PRIO = "text"
+XBUF = 6
+LEAD = 2
+HB = 6
+SB = 4
+EG = 0
+EPRIO = 100000
+LORD = 1
+
+ORDER = [step for j in range(8) for step in ((1, 2 * j), (1, 2 * j + 1), (2, j))] + [(3, j) for j in range(8)]
+STEPS = len(ORDER)
+POS = {kind: i for i, kind in enumerate(ORDER)}
+LAT = {"V": 160, "S": 120, "T": 150, "G": 150, "D": 2000}
+
+
+def list_schedule(tasks):
+    names = list(tasks)
+    rank = {n: tasks[n]["prio"] for n in names}
+    users = {n: [] for n in names}
+    waits = {}
+    for n in names:
+        waits[n] = len(tasks[n]["deps"])
+        for d in tasks[n]["deps"]:
+            users[d].append(n)
+    ready = {n: 0.0 for n in names if waits[n] == 0}
+    at = {n: 0.0 for n in names}
+    free = {e: 0.0 for e in "VSTGD"}
+    last_pe = ""
+    order = []
+    end = 0.0
+    while ready:
+        best = None
+        for n in ready:
+            t = tasks[n]
+            opt = min((max(free[e], at[n]) + c, e) for e, c in t["engs"].items())
+            start = max(free[opt[1]], at[n])
+            key = (start, rank[n])
+            if best is None or key < best[0]:
+                best = (key, n, opt[1])
+        (start, r), n, e = best
+        c = tasks[n]["engs"][e]
+        if e == "T":
+            if last_pe and last_pe != n[0][0]:
+                c += 90
+            last_pe = n[0][0]
+        free[e] = start + c
+        done = start + c + LAT[e]
+        end = max(end, done)
+        order.append((start, n, e))
+        ready.pop(n)
+        for u in users[n]:
+            at[u] = max(at[u], start if tasks[u]["deps"][n] == "order" else done)
+            waits[u] -= 1
+            if waits[u] == 0:
+                ready[u] = at[u]
+    assert len(order) == len(names), [n for n in names if waits[n] > 0][:10]
+    return order
 
 
 def tile_routingassignment_pa_t_w4_kernel(tc, x, adj_bytes, adj_scale, W_words, W_scales, b, out):
     nc = tc.nc
+    tasks = {}
+
+    def task(name, engs, deps, emit, prio=None, after=None):
+        d = {n: "data" for n in deps if n in tasks}
+        if after is not None and after in tasks and after not in d:
+            d[after] = "order"
+        tasks[name] = {"engs": engs, "deps": d, "emit": emit, "prio": prio if prio is not None else len(tasks)}
+
     with ExitStack() as ctx:
         keep = ctx.enter_context(tc.tile_pool(name="keep", bufs=1))
         stream = ctx.enter_context(tc.tile_pool(name="stream", bufs=3))
@@ -36,51 +104,22 @@ def tile_routingassignment_pa_t_w4_kernel(tc, x, adj_bytes, adj_scale, W_words, 
         warm2 = keep.tile([P, 1], F32, name="warm2")
         nc.vector.memset(warm[:], 1.0)
         nc.scalar.activation(out=warm2[:], in_=warm[:], func=ACT.Sqrt)
-
         scale_col = keep.tile([P, 4], F32, name="scale_col")
         with nc.allow_non_contiguous_dma(reason="one scale to a partition"):
             nc.scalar.dma_start(out=scale_col[:], in_=adj_scale.rearrange("a b (m q) -> q (a b m)", q=P))
-
-        x_raw = {}
-
-        def load_x(g):
-            x_raw[g] = stream.tile([P, 4, F], BF16, name="x_raw", bufs=6)
-            nc.sync.dma_start(out=x_raw[g][:], in_=x[g].rearrange("(p t) f -> p t f", t=4))
-
-        adj1 = {}
-
-        def load_adj1(c, g0, g1):
-            t = keep.tile([P, g1 - g0, 2 * N], U8, name="adj1_%d" % c)
-            nc.sync.dma_start(out=t[:], in_=adj_bytes[g0:g1, 0:256, :].rearrange("g (p r) j -> p g (r j)", r=2))
-            for g in range(g0, g1):
-                adj1[g] = (t, g - g0)
-
-        load_x(0)
-        load_adj1(0, 0, 2)
-        load_x(1)
-        load_adj1(1, 2, 4)
-        load_x(2)
         w_sb = keep.tile([P, 2 * K], U8, name="w_sb", align_bytes=64)
-        nc.sync.dma_start(out=w_sb[:], in_=W_words[0])
         w_sc = keep.tile([P, K], U8, name="w_sc", align_bytes=64)
+        b_row = keep.tile([P, K], BF16, name="b_row")
+        ones = keep.tile([P, P], BF16, name="ones")
         ident = keep.tile([P, P], F32, name="ident")
         make_identity(nc, ident[:])
         nc.gpsimd.memset(w_sc[:].bitcast(U32), 0)
-        for q in range(4):
-            nc.sync.dma_start(out=w_sc[32 * q : 32 * q + 4, :].bitcast(I32), in_=W_scales[0, 4 * q : 4 * q + 4, :].bitcast(I32))
-        b_row = keep.tile([P, K], BF16, name="b_row")
         nc.gpsimd.memset(b_row[:], 0.0)
-        ones = keep.tile([P, P], BF16, name="ones")
         nc.gpsimd.memset(ones[:], 1.0)
         nc.scalar.dma_start(out=b_row[0:1, :], in_=b.rearrange("(o c) -> o c", o=1))
-        load_x(3)
-        load_adj1(2, 4, 8)
-        load_x(4)
-        load_x(5)
 
         scale2 = keep.tile([P, 2, N], F32, name="scale2")
         bias2 = keep.tile([P, 2, K], F32, name="bias2")
-
         xc = [keep.tile([P, F], U32, name="xc%d" % g, align_bytes=64) for g in range(G)]
         xs = [keep.tile([P, F], U8, name="xs%d" % g, align_bytes=64) for g in range(G)]
         r1 = keep.tile([P, G, 2, K], F32, name="r1")
@@ -88,246 +127,395 @@ def tile_routingassignment_pa_t_w4_kernel(tc, x, adj_bytes, adj_scale, W_words, 
         r3 = keep.tile([P, G, K], F32, name="r3")
         sum1 = keep.tile([P, G, 2], F32, name="sum1")
         sq1 = keep.tile([P, 2, 8], F32, name="sq1")
+        sum2 = {2: keep.tile([P, G], F32, name="sum2_2"), 3: keep.tile([P, G], F32, name="sum2_3")}
+        sq2 = {2: keep.tile([P, 8], F32, name="sq2_2"), 3: keep.tile([P, 8], F32, name="sq2_3")}
         bst = {2: keep.tile([P, 8, 6], F32, name="bst2"), 3: keep.tile([P, 8, 6], F32, name="bst3")}
         adj2 = keep.tile([P, G, N], U8, name="adj2")
         adj3 = keep.tile([P, G, N], U8, name="adj3")
+        adj1 = {}
 
-        x_grp, sc, psT, ag, ac, asc, psA, gg, gc, gsc, psH, h, ss, rinv = ({} for _ in range(14))
+        x_raw, x_grp, sc, psT, ag, ac, asc, psA, gg, gc, gsc, psH, h, ss, ssm, nrm, rinv = ({} for _ in range(17))
 
         def graphs(s):
-            return (s, s) if s < PH1 else (2 * ((s - PH1) % 8), 2 * ((s - PH1) % 8) + 1)
+            ph, i = ORDER[s]
+            return (i, i) if ph == 1 else (2 * i, 2 * i + 1)
 
-        def x_group(g, half):
-            if half == 0:
-                x_grp[g] = stream.tile([P, 4, P, 4], BF16, name="x_grp", bufs=2, align_bytes=64)
-            m = slice(64 * half, 64 * half + 64)
-            nc.vector.tensor_copy(out=x_grp[g][:].rearrange("p c m t -> p m c t")[:, m], in_=x_raw[g][:].rearrange("p t (m c) -> p m c t", c=4)[:, m])
+        def load_x(g):
+            def emit(e):
+                x_raw[g] = stream.tile([P, 4, F], BF16, name="x_raw", bufs=XBUF)
+                if g == 0:
+                    for hf in range(2):
+                        cols = slice(hf * F // 2, (hf + 1) * F // 2)
+                        nc.sync.dma_start(out=x_raw[g][:, :, cols], in_=x[g].rearrange("(p t) f -> p t f", t=4)[:, :, cols])
+                else:
+                    nc.sync.dma_start(out=x_raw[g][:], in_=x[g].rearrange("(p t) f -> p t f", t=4))
+            task(("lx", g), {"D": 940}, [("xg", g - XBUF, i) for i in range(XPARTS)], emit, after=last_load[0])
+            last_load[0] = ("lx", g)
 
-        def x_quant(g):
-            nc.vector.quantize_mx(out=xc[g][:].bitcast(FP8X4), scales=xs[g][:], in_=x_grp[g][:].rearrange("p c m t -> p (c m t)"))
+        def load_adj1(c, g0, g1):
+            def emit(e):
+                t = keep.tile([P, g1 - g0, 2 * N], U8, name="adj1_%d" % c)
+                nc.sync.dma_start(out=t[:], in_=adj_bytes[g0:g1, 0:256, :].rearrange("g (p r) j -> p g (r j)", r=2))
+                for g in range(g0, g1):
+                    adj1[g] = (t, g - g0)
+            task(("la", c), {"D": 250 * (g1 - g0)}, [], emit, after=last_load[0])
+            last_load[0] = ("la", c)
+            for g in range(g0, g1):
+                la_of[1, g] = ("la", c)
 
-        def adj_scale_mul(s):
-            sc[s] = stream.tile([P, 2 * N], BF16, name="sc", align_bytes=64)
-            if s < PH1:
-                t, i = adj1[s]
-                src = t[:, i, :]
-            else:
+        def load_adj23(ph):
+            t, n0 = (adj2, 256) if ph == 2 else (adj3, 384)
+
+            def emit(e):
+                nc.sync.dma_start(out=t[:], in_=adj_bytes[:, n0 : n0 + P, :].rearrange("g p j -> p g j"))
+            task(("la", 10 + ph), {"D": 2500}, [], emit, after=last_load[0])
+            last_load[0] = ("la", 10 + ph)
+            for j in range(8):
+                la_of[ph, j] = ("la", 10 + ph)
+
+        la_of = {}
+        last_load = [None]
+
+        def load_w(e):
+            nc.sync.dma_start(out=w_sb[:], in_=W_words[0])
+            for q in range(4):
+                nc.sync.dma_start(out=w_sc[32 * q : 32 * q + 4, :].bitcast(I32), in_=W_scales[0, 4 * q : 4 * q + 4, :].bitcast(I32))
+
+        def t_x_group(g, i):
+            m = slice(i * P // XPARTS, (i + 1) * P // XPARTS)
+
+            def emit(e):
+                if i == 0:
+                    x_grp[g] = stream.tile([P, 4, P, 4], BF16, name="x_grp", bufs=3, align_bytes=64)
+                o = x_grp[g][:].rearrange("p c m t -> p m c t")[:, m]
+                n = x_raw[g][:].rearrange("p t (m c) -> p m c t", c=4)[:, m]
+                if e == "V":
+                    nc.vector.tensor_copy(out=o, in_=n)
+                else:
+                    nc.scalar.copy(out=o, in_=n)
+            engs = {"V": 16 + 1126 / XPARTS}
+            if XS:
+                engs["S"] = 12 + 2000 / XPARTS
+            task(("xg", g, i), engs, [("lx", g), ("xq", g - 3)], emit, after=("xg", g - 1, XPARTS - 1) if i == 0 else ("xg", g, i - 1))
+
+        def t_x_quant(g):
+            def emit(e):
+                nc.vector.quantize_mx(out=xc[g][:].bitcast(FP8X4), scales=xs[g][:], in_=x_grp[g][:].rearrange("p c m t -> p (c m t)"))
+            task(("xq", g), {"V": 467}, [("xg", g, i) for i in range(XPARTS)], emit)
+
+        def t_scale(s):
+            def emit(e):
+                sc[s] = stream.tile([P, 2 * N], BF16, name="sc", bufs=SB, align_bytes=64)
                 g0, g1 = graphs(s)
-                src = (adj2 if s < PH2 else adj3)[:, g0 : g1 + 1, :].rearrange("p g j -> p (g j)")
-            nc.vector.tensor_tensor(out=sc[s][:], in0=src.bitcast(FP8), in1=scale2[:].rearrange("p a j -> p (a j)"), op=ALU.mult)
+                if ORDER[s][0] == 1:
+                    t, i = adj1[g0]
+                    src = t[:, i, :]
+                else:
+                    src = (adj2 if ORDER[s][0] == 2 else adj3)[:, g0 : g1 + 1, :].rearrange("p g j -> p (g j)")
+                nc.vector.tensor_tensor(out=sc[s][:], in0=src.bitcast(FP8), in1=scale2[:].rearrange("p a j -> p (a j)"), op=ALU.mult)
+            task(("sc", s), {"V": 872}, [la_of[ORDER[s]], ("scale", 0), ("T", s - SB)], emit, after=("sc", s - 1))
 
-        def adj_transpose(s):
-            psT[s] = psum.tile([P, 2, 2, P], F32, name="psT", bufs=2)
-            words = sc[s][:].bitcast(F32)
-            for a in range(2):
-                for u in range(2):
-                    nc.tensor.transpose(psT[s][:, a, u, :], words[:, 256 * a + u : 256 * (a + 1) : 2], ident[:])
+        def t_transpose(s):
+            def emit(e):
+                psT[s] = psum.tile([P, 2, 2, P], F32, name="psT", bufs=2)
+                words = sc[s][:].bitcast(F32)
+                for a in range(2):
+                    for u in range(2):
+                        nc.tensor.transpose(psT[s][:, a, u, :], words[:, 256 * a + u : 256 * (a + 1) : 2], ident[:])
+            task(("T", s), {"T": 760}, [("sc", s), ("te", s - 2)], emit, after=("T", s - 1))
 
-        def adj_exit(s):
-            ag[s] = stream.tile([P, 8 * P], BF16, name="ag", align_bytes=64)
-            nc.scalar.copy(out=ag[s][:].bitcast(F32).rearrange("p (a n u) -> p a n u", a=2, u=2), in_=psT[s][:].rearrange("p a u n -> p a n u"))
+        def copy(e, o, n):
+            if e == "V":
+                nc.vector.tensor_copy(out=o, in_=n)
+            else:
+                nc.scalar.copy(out=o, in_=n)
 
-        def adj_quant(s):
-            ac[s] = stream.tile([P, 2 * P], U32, name="ac", align_bytes=64)
-            asc[s] = stream.tile([P, 2 * P], U8, name="asc", align_bytes=64)
-            nc.vector.quantize_mx(out=ac[s][:].bitcast(FP8X4), scales=asc[s][:], in_=ag[s][:])
+        def t_adj_exit(s):
+            def emit(e):
+                ag[s] = stream.tile([P, 8 * P], BF16, name="ag", bufs=SB, align_bytes=64)
+                copy(e, ag[s][:].bitcast(F32).rearrange("p (a n u) -> p a n u", a=2, u=2), psT[s][:].rearrange("p a u n -> p a n u"))
+            engs = {"S": 440, "V": 444} if EXV else {"S": 440}
+            task(("te", s), engs, [("T", s), ("q", s - SB)], emit, after=("te", s - 1))
 
-        def agg_matmul(s):
-            gr = graphs(s)
-            for a in range(2):
+        def t_adj_quant(s):
+            def emit(e):
+                ac[s] = stream.tile([P, 2 * P], U32, name="ac", bufs=SB, align_bytes=64)
+                asc[s] = stream.tile([P, 2 * P], U8, name="asc", bufs=SB, align_bytes=64)
+                nc.vector.quantize_mx(out=ac[s][:].bitcast(FP8X4), scales=asc[s][:], in_=ag[s][:])
+            task(("q", s), {"V": 241}, [("te", s), ("M", s - SB, 1)], emit, after=("q", s - 1))
+
+        def t_agg(s, a):
+            def emit(e):
+                g = graphs(s)[a]
                 psA[s, a] = psum.tile([P, 4, P], F32, name="psA", bufs=4)
                 rows = slice(P * a, P * (a + 1))
                 for t in range(4):
                     cols = slice(P * t, P * (t + 1))
                     nc.tensor.matmul_mx(
                         out=psA[s, a][:, t, :],
-                        lhsT=xc[gr[a]][:, cols].bitcast(FP8X4), lhsT_scale=xs[gr[a]][:, cols],
+                        lhsT=xc[g][:, cols].bitcast(FP8X4), lhsT_scale=xs[g][:, cols],
                         rhs=ac[s][:, rows].bitcast(FP8X4), rhs_scale=asc[s][:, rows],
                         start=True, stop=True)
+            task(("M", s, a), {"T": 455}, [("q", s), ("xq", graphs(s)[a]), ("ae", s - 2, a)], emit, after=("M", s, 0) if a else ("M", s - 1, 1))
 
-        def agg_exit(s):
-            gg[s] = stream.tile([P, 2, P, 4], BF16, name="gg", align_bytes=64)
-            for a in range(2):
-                nc.scalar.copy(out=gg[s][:, a], in_=psA[s, a][:].rearrange("p t n -> p n t"))
+        def t_agg_exit(s, a):
+            def emit(e):
+                if a == 0:
+                    gg[s] = stream.tile([P, 2, P, 4], BF16, name="gg", bufs=SB, align_bytes=64)
+                copy(e, gg[s][:, a], psA[s, a][:].rearrange("p t n -> p n t"))
+            engs = {"S": 440, "V": 444} if EXV else {"S": 440}
+            task(("ae", s, a), engs, [("M", s, a), ("qa", s - SB)], emit, after=("ae", s, 0) if a else ("ae", s - 1, 1))
 
-        def agg_quant(s):
-            gc[s] = stream.tile([P, 2 * P], U32, name="gc", align_bytes=64)
-            gsc[s] = stream.tile([P, 2 * P], U8, name="gsc", align_bytes=64)
-            nc.vector.quantize_mx(out=gc[s][:].bitcast(FP8X4), scales=gsc[s][:], in_=gg[s][:].rearrange("p a n t -> p (a n t)"))
+        def t_agg_quant(s):
+            def emit(e):
+                gc[s] = stream.tile([P, 2 * P], U32, name="gc", bufs=SB, align_bytes=64)
+                gsc[s] = stream.tile([P, 2 * P], U8, name="gsc", bufs=SB, align_bytes=64)
+                nc.vector.quantize_mx(out=gc[s][:].bitcast(FP8X4), scales=gsc[s][:], in_=gg[s][:].rearrange("p a n t -> p (a n t)"))
+            task(("qa", s), {"V": 241}, [("ae", s, 0), ("ae", s, 1), ("H", s - SB)], emit, after=("qa", s - 1))
 
-        def h_matmul(s):
-            psH[s] = psum.tile([P, 2, K], F32, name="psH", bufs=2)
-            for a in range(2):
-                rows = slice(P * a, P * (a + 1))
-                nc.tensor.matmul_mx(
-                    out=psH[s][:, a, :],
-                    lhsT=gc[s][:, rows].bitcast(FP8X4), lhsT_scale=gsc[s][:, rows],
-                    rhs=w_sb[:].bitcast(FP4X4), rhs_scale=w_sc[:],
-                    start=True, stop=True)
+        def t_h(s):
+            def emit(e):
+                psH[s] = psum.tile([P, 2, K], F32, name="psH", bufs=2)
+                for a in range(2):
+                    rows = slice(P * a, P * (a + 1))
+                    nc.tensor.matmul_mx(
+                        out=psH[s][:, a, :],
+                        lhsT=gc[s][:, rows].bitcast(FP8X4), lhsT_scale=gsc[s][:, rows],
+                        rhs=w_sb[:].bitcast(FP4X4), rhs_scale=w_sc[:],
+                        start=True, stop=True)
+            task(("H", s), {"T": 445}, [("qa", s), ("lw", 0), ("A", s - 2)], emit, after=("H", s - 1))
 
-        def h_bias(s):
-            h[s] = stream.tile([P, 2, K], F32, name="h", bufs=5)
-            nc.vector.tensor_tensor(out=h[s][:], in0=psH[s][:], in1=bias2[:], op=ALU.add)
+        def t_bias(s):
+            def emit(e):
+                h[s] = stream.tile([P, 2, K], F32, name="h", bufs=HB)
+                nc.vector.tensor_tensor(out=h[s][:], in0=psH[s][:], in1=bias2[:], op=ALU.add)
+            task(("A", s), {"V": 444}, [("H", s), ("bias", 0), ("C", s - HB, 0), ("C", s - HB, 1)], emit, after=("A", s - 1))
 
-        def h_square(s):
-            if s % 2 == 0:
-                ss[s // 2] = stream.tile([P, 4], F32, name="ss")
-            for a in range(2):
+        def t_square(s, a):
+            def emit(e):
+                if s % 2 == 0 and a == 0:
+                    ss[s // 2] = stream.tile([P, 4], F32, name="ss")
                 junk = stream.tile([P, K], F32, name="junk", bufs=2)
                 col = 2 * (s % 2) + a
                 nc.scalar.activation(out=junk[:], in_=h[s][:, a, :], func=ACT.Square, accum_out=ss[s // 2][:, col : col + 1])
+            task(("B", s, a), {"S": 246}, [("A", s)], emit, after=("B", s, 0) if a else ("B", s - 1, 1))
 
-        def norm_root(m):
-            ssm = stream.tile([P, 4], F32, name="ssm")
-            nc.gpsimd.tensor_scalar(out=ssm[:], in0=ss[m][:], scalar1=NORM_EPS * NORM_EPS, scalar2=None, op0=ALU.max)
-            rinv[m] = stream.tile([P, 4], F32, name="rinv")
-            nrm = stream.tile([P, 4], F32, name="nrm")
-            nc.scalar.activation(out=nrm[:], in_=ssm[:], func=ACT.Sqrt)
-            ss[m] = nrm
+        def t_norm(m):
+            def emit_max(e):
+                ssm[m] = stream.tile([P, 4], F32, name="ssm")
+                nc.gpsimd.tensor_scalar(out=ssm[m][:], in0=ss[m][:], scalar1=NORM_EPS * NORM_EPS, scalar2=None, op0=ALU.max)
 
-        def norm_recip(m):
-            nc.vector.reciprocal(out=rinv[m][:], in_=ss[m][:])
+            def emit_sqrt(e):
+                nrm[m] = stream.tile([P, 4], F32, name="nrm")
+                nc.scalar.activation(out=nrm[m][:], in_=ssm[m][:], func=ACT.Sqrt)
 
-        def relu(s):
-            g0, g1 = graphs(s)
-            for a in range(2):
-                sc_ap = rinv[s // 2][:, 2 * (s % 2) + a : 2 * (s % 2) + a + 1]
-                if s < PH1:
-                    nc.scalar.activation(out=r1[:, g0, a, :], in_=h[s][:, a, :], func=ACT.Relu, scale=sc_ap, accum_out=sum1[:, g0, a : a + 1])
+            def emit_recip(e):
+                rinv[m] = stream.tile([P, 4], F32, name="rinv")
+                nc.vector.reciprocal(out=rinv[m][:], in_=nrm[m][:])
+            task(("n1", m), {"G": 125}, [("B", s, a) for s in (2 * m, 2 * m + 1) for a in (0, 1)], emit_max, after=("n1", m - 1))
+            task(("n2", m), {"S": 45}, [("n1", m)], emit_sqrt, after=("n2", m - 1))
+            task(("n3", m), {"V": 55}, [("n2", m)], emit_recip, after=("n3", m - 1))
+
+        def t_relu(s, a):
+            ph, i = ORDER[s]
+
+            def emit(e):
+                g0, g1 = graphs(s)
+                f = rinv[s // 2][:, 2 * (s % 2) + a : 2 * (s % 2) + a + 1]
+                if ph == 1:
+                    dst, acc = r1[:, g0, a, :], sum1[:, g0, a : a + 1]
                 else:
-                    dst = r2 if s < PH2 else r3
-                    nc.scalar.activation(out=dst[:, g0 + a, :], in_=h[s][:, a, :], func=ACT.Relu, scale=sc_ap)
+                    dst, acc = (r2 if ph == 2 else r3)[:, g0 + a, :], sum2[ph][:, g0 + a : g0 + a + 1]
+                if e == "V":
+                    nc.vector.tensor_scalar(out=dst, in0=h[s][:, a, :], scalar1=f, scalar2=0.0, op0=ALU.mult, op1=ALU.max)
+                elif ph in BN:
+                    nc.scalar.activation(out=dst, in_=h[s][:, a, :], func=ACT.Relu, scale=f)
+                else:
+                    nc.scalar.activation(out=dst, in_=h[s][:, a, :], func=ACT.Relu, scale=f, accum_out=acc)
+            engs = {"S": 231, "V": 124} if ph in BN else {"S": 250}
+            task(("C", s, a), engs, [("n3", s // 2)], emit, after=("C", s, 0) if a else ("C", s - 1, 1))
 
-        def sq_sum1(j, a):
-            junk2 = stream.tile([P, 2, K], F32, name="junk2", bufs=2)
-            nc.scalar.activation(out=junk2[:], in_=r1[:, 2 * j : 2 * j + 2, a, :], func=ACT.Square, accum_out=sq1[:, a, j : j + 1])
+        def t_sum_squares(ph, j, a):
+            def emit(e):
+                t = r1[:, 2 * j : 2 * j + 2, a, :] if ph == 1 else (r2 if ph == 2 else r3)[:, 2 * j : 2 * j + 2, :]
+                if ph in BN:
+                    nc.vector.bn_stats(out=bst[ph][:, j, :], in_=t.rearrange("p g c -> p (g c)"))
+                else:
+                    junk2 = stream.tile([P, 2, K], F32, name="junk2", bufs=2)
+                    nc.scalar.activation(out=junk2[:], in_=t, func=ACT.Square, accum_out=sq1[:, a, j : j + 1] if ph == 1 else sq2[ph][:, j : j + 1])
+            deps = [("C", POS[1, g], a) for g in (2 * j, 2 * j + 1)] if ph == 1 else [("C", POS[ph, j], c) for c in (0, 1)]
+            task(("D", ph, j, a), {"V": 444} if ph in BN else {"S": 459}, deps, emit)
 
-        def stats23(s):
-            g0, g1 = graphs(s)
-            src = r2 if s < PH2 else r3
-            i = (s - PH1) % 8
-            nc.vector.bn_stats(out=bst[2 if s < PH2 else 3][:, i, :], in_=src[:, g0 : g1 + 1, :].rearrange("p g c -> p (g c)"))
+        coef = {}
 
-        mean, root, coef = {}, {}, {}
-
-        def finish_a(ph):
+        def t_finish(ph):
             n = 2 if ph == 1 else 1
-            varp = keep.tile([P, n], F32, name="varp%d" % ph)
-            if ph == 1:
-                mean[1] = keep.tile([P, 2], F32, name="mean1")
-                e2 = keep.tile([P, 2], F32, name="e2")
-                m2 = keep.tile([P, 2], F32, name="m2")
-                nc.vector.tensor_reduce(out=mean[1][:], in_=sum1[:].rearrange("p g a -> p a g"), axis=AXX, op=ALU.add)
-                nc.vector.tensor_reduce(out=e2[:], in_=sq1[:], axis=AXX, op=ALU.add)
-                nc.vector.tensor_scalar(out=mean[1][:], in0=mean[1][:], scalar1=1.0 / (G * K), scalar2=None, op0=ALU.mult)
-                nc.vector.tensor_tensor(out=m2[:], in0=mean[1][:], in1=mean[1][:], op=ALU.mult)
-                nc.vector.scalar_tensor_tensor(out=varp[:], in0=e2[:], scalar=1.0 / (G * K), in1=m2[:], op0=ALU.mult, op1=ALU.subtract)
-                nc.vector.tensor_scalar(out=varp[:], in0=varp[:], scalar1=BN_EPS, scalar2=None, op0=ALU.add)
-            else:
-                mv = keep.tile([P, 2], F32, name="mv%d" % ph)
-                nc.vector.bn_aggr(out=mv[:], in_=bst[ph][:].rearrange("p i s -> p (i s)"))
-                mean[ph] = mv
-                nc.vector.tensor_scalar(out=varp[:], in0=mv[:, 1:2], scalar1=BN_EPS, scalar2=None, op0=ALU.add)
-            root[ph] = keep.tile([P, n], F32, name="root%d" % ph)
-            nc.scalar.activation(out=root[ph][:], in_=varp[:], func=ACT.Sqrt)
+            st = {}
 
-        def finish_b(ph):
-            n = 2 if ph == 1 else 1
-            a = keep.tile([P, n], F32, name="a%d" % ph)
-            c = keep.tile([P, n], F32, name="c%d" % ph)
-            nc.vector.reciprocal(out=a[:], in_=root[ph][:])
-            nc.vector.scalar_tensor_tensor(out=c[:], in0=mean[ph][:, 0:n], scalar=-1.0, in1=a[:], op0=ALU.mult, op1=ALU.mult)
-            coef[ph] = (a, c)
+            def emit_var(e):
+                varp = keep.tile([P, n], F32, name="varp%d" % ph)
+                if ph not in BN:
+                    mean = keep.tile([P, n], F32, name="mean%d" % ph)
+                    e2 = keep.tile([P, n], F32, name="e2_%d" % ph)
+                    m2 = keep.tile([P, n], F32, name="m2_%d" % ph)
+                    nc.vector.tensor_reduce(out=mean[:], in_=sum1[:].rearrange("p g a -> p a g") if ph == 1 else sum2[ph][:], axis=AXX, op=ALU.add)
+                    nc.vector.tensor_reduce(out=e2[:], in_=sq1[:] if ph == 1 else sq2[ph][:], axis=AXX, op=ALU.add)
+                    nc.vector.tensor_scalar(out=mean[:], in0=mean[:], scalar1=1.0 / (G * K), scalar2=None, op0=ALU.mult)
+                    nc.vector.tensor_tensor(out=m2[:], in0=mean[:], in1=mean[:], op=ALU.mult)
+                    nc.vector.scalar_tensor_tensor(out=varp[:], in0=e2[:], scalar=1.0 / (G * K), in1=m2[:], op0=ALU.mult, op1=ALU.subtract)
+                    nc.vector.tensor_scalar(out=varp[:], in0=varp[:], scalar1=BN_EPS, scalar2=None, op0=ALU.add)
+                else:
+                    mean = keep.tile([P, 2], F32, name="mv%d" % ph)
+                    nc.vector.bn_aggr(out=mean[:], in_=bst[ph][:].rearrange("p i s -> p (i s)"))
+                    nc.vector.tensor_scalar(out=varp[:], in0=mean[:, 1:2], scalar1=BN_EPS, scalar2=None, op0=ALU.add)
+                st["mean"], st["varp"] = mean, varp
 
-        def emit(ph, q, i):
-            a, c = coef[ph]
+            def emit_sqrt(e):
+                st["root"] = keep.tile([P, n], F32, name="root%d" % ph)
+                nc.scalar.activation(out=st["root"][:], in_=st["varp"][:], func=ACT.Sqrt)
+
+            def emit_coef(e):
+                cf = keep.tile([P, n, 2], F32, name="coef%d" % ph)
+                nc.vector.reciprocal(out=cf[:, :, 0], in_=st["root"][:])
+                nc.vector.scalar_tensor_tensor(out=cf[:, :, 1], in0=st["mean"][:, 0:n], scalar=-1.0, in1=cf[:, :, 0], op0=ALU.mult, op1=ALU.mult)
+                coef[ph] = cf
+            task(("f1", ph), {"V": 420 if ph in BN else 900}, [("D", ph, j, a) for j in range(8) for a in range(n)], emit_var)
+            task(("f2", ph), {"S": 45}, [("f1", ph)], emit_sqrt)
+            task(("f3", ph), {"V": 270}, [("f2", ph)], emit_coef)
+
+        def t_affine(ph, q, i):
             g4 = slice(4 * q, 4 * q + 4)
-            t = r1[:, g4, i, :] if ph == 1 else (r2 if ph == 2 else r3)[:, g4, :]
-            nc.vector.tensor_scalar(out=t, in0=t, scalar1=a[:, i : i + 1], scalar2=c[:, i : i + 1], op0=ALU.mult, op1=ALU.add)
-            if ph == 1 and i == 1:
-                nc.sync.dma_start(out=out[g4, 0:256, :].rearrange("g (p r) c -> p g (r c)", r=2), in_=r1[:, g4].rearrange("p g r c -> p g (r c)"))
-            if ph > 1:
-                n0 = 256 if ph == 2 else 384
-                nc.sync.dma_start(out=out[g4, n0 : n0 + P, :].rearrange("g p c -> p g c"), in_=t)
 
-        todo = []
+            def emit(e):
+                t = r1[:, g4, i, :] if ph == 1 else (r2 if ph == 2 else r3)[:, g4, :]
+                a, c = coef[ph][:, i, 0:1], coef[ph][:, i, 1:2]
+                if e == "S":
+                    nc.scalar.activation(out=t, in_=t, func=ACT.Identity, scale=a, bias=c)
+                elif e == "V":
+                    nc.vector.tensor_scalar(out=t, in0=t, scalar1=a, scalar2=c, op0=ALU.mult, op1=ALU.add)
+                else:
+                    nc.gpsimd.tensor_scalar(out=t, in0=t, scalar1=a, scalar2=c, op0=ALU.mult, op1=ALU.add)
+            engs = {"V": 446, "S": 875}
+            if EG:
+                engs["G"] = 1150
+            task(("E", ph, q, i), engs, [("f3", ph)], emit, prio=(EPRIO + 8 * ph + 2 * q + i) if ph < 3 else None)
 
-        with tc.manual_schedule():
+        def t_store(ph, q):
+            g4 = slice(4 * q, 4 * q + 4)
+
+            def emit(e):
+                if ph == 1:
+                    nc.sync.dma_start(out=out[g4, 0:256, :].rearrange("g (p r) c -> p g (r c)", r=2), in_=r1[:, g4].rearrange("p g r c -> p g (r c)"))
+                else:
+                    n0 = 256 if ph == 2 else 384
+                    nc.sync.dma_start(out=out[g4, n0 : n0 + P, :].rearrange("g p c -> p g c"), in_=(r2 if ph == 2 else r3)[:, g4, :])
+            task(("st", ph, q), {"D": 1900 if ph == 1 else 950}, [("E", ph, q, i) for i in range(2 if ph == 1 else 1)], emit)
+
+        def emit_scale(e):
             psc = psum.tile([P, 4, P], F32, name="psA", bufs=4)
             for m in range(4):
                 nc.tensor.transpose(psc[:, m, :], scale_col[:, m : m + 1].to_broadcast([P, P]), ident[:])
-            x_group(0, 0)
-            x_group(0, 1)
             nc.scalar.copy(out=scale2[:, 0, :], in_=psc[:].rearrange("p m q -> p (m q)"))
             nc.scalar.copy(out=scale2[:, 1, :], in_=psc[:].rearrange("p m q -> p (m q)"))
-            adj_scale_mul(0)
-            x_quant(0)
+
+        def emit_bias(e):
             psb = psum.tile([P, 2, K], F32, name="psH", bufs=2)
             for a in range(2):
                 nc.tensor.matmul(psb[:, a, :], lhsT=ones[:], rhs=b_row[:], start=True, stop=True)
             nc.scalar.copy(out=bias2[:], in_=psb[:])
 
-            for k in range(STEPS + 8):
-                if k + 6 < G:
-                    load_x(k + 6)
-                if k == 1:
+        task(("scale0", 0), {"D": 2600}, [], lambda e: None)
+        tasks.pop(("scale0", 0))
+        tasks[("boot", 0)] = {"engs": {"S": 4760}, "deps": {}, "emit": lambda e: None, "prio": -1}
+        task(("scale1", 0), {"T": 760}, [("boot", 0)], lambda e: None)
+        task(("scale", 0), {"S": 880}, [("scale1", 0)], emit_scale)
+        task(("bias", 0), {"S": 440}, [("scale", 0)], emit_bias)
+
+        load_x(0)
+        if LORD:
+            load_x(1)
+            load_adj1(0, 0, 2)
+        else:
+            load_adj1(0, 0, 2)
+            load_x(1)
+        load_x(2)
+        load_adj1(1, 2, 4)
+        task(("lw", 0), {"D": 600}, [], load_w, after=last_load[0])
+        load_x(3)
+        load_adj1(2, 4, 8)
+        load_x(4)
+        load_x(5)
+        done_x = 0
+        next_load = [6]
+
+        def do_x(g):
+            for i in range(XPARTS):
+                t_x_group(g, i)
+            t_x_quant(g)
+            if next_load[0] < G:
+                load_x(next_load[0])
+                next_load[0] += 1
+                if next_load[0] == 9:
                     load_adj1(3, 8, 16)
-                if k == 9:
-                    nc.sync.dma_start(out=adj2[:], in_=adj_bytes[:, 256:384, :].rearrange("g p j -> p g j"))
-                    nc.sync.dma_start(out=adj3[:], in_=adj_bytes[:, 384:512, :].rearrange("g p j -> p g j"))
+                if next_load[0] == (7 if MIX else 13):
+                    load_adj23(2)
+                if next_load[0] == 15:
+                    load_adj23(3)
+
+        for k in range(-1, STEPS + 8):
+            if k >= 0:
                 if k < STEPS:
-                    adj_transpose(k)
+                    t_transpose(k)
+                    t_adj_exit(k)
                 if 0 <= k - 1 < STEPS:
-                    adj_quant(k - 1)
+                    t_adj_quant(k - 1)
+                    for a in range(2):
+                        t_agg(k - 1, a)
+                        t_agg_exit(k - 1, a)
                 if 0 <= k - 2 < STEPS:
-                    agg_quant(k - 2)
-                if 0 <= k - 1 < STEPS:
-                    agg_matmul(k - 1)
-                if 0 <= k - 2 < STEPS:
-                    h_matmul(k - 2)
-                if k % 2 == 1 and 0 <= k - 5 < STEPS:
-                    norm_recip((k - 5) // 2)
-                if k + 1 < G:
-                    x_group(k + 1, 0)
-                if k + 1 < STEPS:
-                    adj_scale_mul(k + 1)
-                if k + 1 < G:
-                    x_group(k + 1, 1)
-                if 0 <= k - 2 < STEPS:
-                    h_bias(k - 2)
-                if k + 1 < G:
-                    x_quant(k + 1)
+                    t_agg_quant(k - 2)
+                    t_h(k - 2)
+                    t_bias(k - 2)
                 if 0 <= k - 3 < STEPS:
-                    h_square(k - 3)
-                if k < STEPS:
-                    adj_exit(k)
-                if 0 <= k - 1 < STEPS:
-                    agg_exit(k - 1)
-                if k % 2 == 0 and 0 <= k - 4 < STEPS:
-                    norm_root((k - 4) // 2)
+                    for a in range(2):
+                        t_square(k - 3, a)
+                    if (k - 3) % 2 == 1:
+                        t_norm((k - 3) // 2)
                 if 0 <= k - 5 < STEPS:
-                    relu(k - 5)
-                if k % 2 == 0 and 0 <= k - 6 < PH1:
-                    sq_sum1((k - 6) // 2, 0)
-                if k % 2 == 1 and 0 <= k - 7 < PH1:
-                    sq_sum1((k - 7) // 2, 1)
-                if PH1 <= k - 6 < STEPS:
-                    stats23(k - 6)
-                if todo:
-                    emit(*todo.pop(0))
-                if k == PH1 + 6:
-                    finish_a(1)
-                if k == PH1 + 7:
-                    finish_b(1)
-                    todo += [(1, q, i) for q in range(4) for i in range(2)]
-                if k == PH2 + 5:
-                    finish_a(2)
-                if k == PH2 + 6:
-                    finish_b(2)
-                    todo += [(2, q, 0) for q in range(4)]
-            finish_a(3)
-            for e in todo:
-                emit(*e)
-            finish_b(3)
-            for q in range(4):
-                emit(3, q, 0)
+                    for a in range(2):
+                        t_relu(k - 5, a)
+                    ph, i = ORDER[k - 5]
+                    if ph > 1:
+                        t_sum_squares(ph, i, 0)
+                    elif i % 2 == 1:
+                        t_sum_squares(1, i // 2, 0)
+                        t_sum_squares(1, i // 2, 1)
+                for ph, last in ((1, (1, 15)), (2, (2, 7)), (3, (3, 7))):
+                    if k - 6 == POS[last]:
+                        t_finish(ph)
+                        for q in range(4):
+                            for i in range(2 if ph == 1 else 1):
+                                t_affine(ph, q, i)
+                            t_store(ph, q)
+            while done_x < G and k + LEAD >= POS[1, done_x]:
+                do_x(done_x)
+                done_x += 1
+            if k + 1 < STEPS:
+                t_scale(k + 1)
+
+        if PRIO == "bottom":
+            names = list(tasks)
+            users = {n: [] for n in names}
+            for n in names:
+                for d in tasks[n]["deps"]:
+                    users[d].append(n)
+            level = {}
+            for n in reversed(names):
+                t = tasks[n]
+                level[n] = min(t["engs"].values()) + max([level[u] + 150 for u in users[n]] + [0])
+            for n in names:
+                tasks[n]["prio"] = -level[n]
+        order = list_schedule(tasks)
+        with tc.manual_schedule():
+            for start, n, e in sorted(order, key=lambda r: r[0]):
+                tasks[n]["emit"](e)

@@ -21,21 +21,22 @@ ACT = mybir.ActivationFunctionType
 ALU = mybir.AluOpType
 AXX = mybir.AxisListType.X
 
-MIX = 1
 BN = (2, 3)
 XPARTS = 4
 XS = 1
-EXV = 0
 PRIO = "text"
 XBUF = 6
-LEAD = 2
+LEAD = 1
 HB = 6
 SB = 4
 EG = 0
 EPRIO = 100000
-LORD = 1
+CXS = 3000
+CXV = 1126
+CT = 1000
+CACC = 50
 
-ORDER = [step for j in range(8) for step in ((1, 2 * j), (1, 2 * j + 1), (2, j))] + [(3, j) for j in range(8)]
+ORDER = [step for j in range(8) for step in ((1, 2 * j), (1, 2 * j + 1)) + (((2, j - 1),) if j > 0 else ())] + [(2, 7)] + [(3, j) for j in range(8)]
 STEPS = len(ORDER)
 POS = {kind: i for i, kind in enumerate(ORDER)}
 LAT = {"V": 160, "S": 120, "T": 150, "G": 150, "D": 2000}
@@ -163,15 +164,16 @@ def tile_routingassignment_pa_t_w4_kernel(tc, x, adj_bytes, adj_scale, W_words, 
             for g in range(g0, g1):
                 la_of[1, g] = ("la", c)
 
-        def load_adj23(ph):
+        def load_adj23(ph, j0, j1):
             t, n0 = (adj2, 256) if ph == 2 else (adj3, 384)
+            gs = slice(2 * j0, 2 * j1)
 
             def emit(e):
-                nc.sync.dma_start(out=t[:], in_=adj_bytes[:, n0 : n0 + P, :].rearrange("g p j -> p g j"))
-            task(("la", 10 + ph), {"D": 2500}, [], emit, after=last_load[0])
-            last_load[0] = ("la", 10 + ph)
-            for j in range(8):
-                la_of[ph, j] = ("la", 10 + ph)
+                nc.sync.dma_start(out=t[:, gs, :], in_=adj_bytes[gs, n0 : n0 + P, :].rearrange("g p j -> p g j"))
+            task(("lb", ph, j0), {"D": 400 * (j1 - j0)}, [], emit, after=last_load[0])
+            last_load[0] = ("lb", ph, j0)
+            for j in range(j0, j1):
+                la_of[ph, j] = ("lb", ph, j0)
 
         la_of = {}
         last_load = [None]
@@ -193,9 +195,9 @@ def tile_routingassignment_pa_t_w4_kernel(tc, x, adj_bytes, adj_scale, W_words, 
                     nc.vector.tensor_copy(out=o, in_=n)
                 else:
                     nc.scalar.copy(out=o, in_=n)
-            engs = {"V": 16 + 1126 / XPARTS}
+            engs = {"V": 16 + CXV / XPARTS}
             if XS:
-                engs["S"] = 12 + 2000 / XPARTS
+                engs["S"] = 12 + CXS / XPARTS
             task(("xg", g, i), engs, [("lx", g), ("xq", g - 3)], emit, after=("xg", g - 1, XPARTS - 1) if i == 0 else ("xg", g, i - 1))
 
         def t_x_quant(g):
@@ -222,7 +224,7 @@ def tile_routingassignment_pa_t_w4_kernel(tc, x, adj_bytes, adj_scale, W_words, 
                 for a in range(2):
                     for u in range(2):
                         nc.tensor.transpose(psT[s][:, a, u, :], words[:, 256 * a + u : 256 * (a + 1) : 2], ident[:])
-            task(("T", s), {"T": 760}, [("sc", s), ("te", s - 2)], emit, after=("T", s - 1))
+            task(("T", s), {"T": CT}, [("sc", s), ("te", s - 2)], emit, after=("T", s - 1))
 
         def copy(e, o, n):
             if e == "V":
@@ -234,7 +236,7 @@ def tile_routingassignment_pa_t_w4_kernel(tc, x, adj_bytes, adj_scale, W_words, 
             def emit(e):
                 ag[s] = stream.tile([P, 8 * P], BF16, name="ag", bufs=SB, align_bytes=64)
                 copy(e, ag[s][:].bitcast(F32).rearrange("p (a n u) -> p a n u", a=2, u=2), psT[s][:].rearrange("p a u n -> p a n u"))
-            engs = {"S": 440, "V": 444} if EXV else {"S": 440}
+            engs = {"S": 440}
             task(("te", s), engs, [("T", s), ("q", s - SB)], emit, after=("te", s - 1))
 
         def t_adj_quant(s):
@@ -263,7 +265,7 @@ def tile_routingassignment_pa_t_w4_kernel(tc, x, adj_bytes, adj_scale, W_words, 
                 if a == 0:
                     gg[s] = stream.tile([P, 2, P, 4], BF16, name="gg", bufs=SB, align_bytes=64)
                 copy(e, gg[s][:, a], psA[s, a][:].rearrange("p t n -> p n t"))
-            engs = {"S": 440, "V": 444} if EXV else {"S": 440}
+            engs = {"S": 440}
             task(("ae", s, a), engs, [("M", s, a), ("qa", s - SB)], emit, after=("ae", s, 0) if a else ("ae", s - 1, 1))
 
         def t_agg_quant(s):
@@ -298,7 +300,7 @@ def tile_routingassignment_pa_t_w4_kernel(tc, x, adj_bytes, adj_scale, W_words, 
                 junk = stream.tile([P, K], F32, name="junk", bufs=2)
                 col = 2 * (s % 2) + a
                 nc.scalar.activation(out=junk[:], in_=h[s][:, a, :], func=ACT.Square, accum_out=ss[s // 2][:, col : col + 1])
-            task(("B", s, a), {"S": 246}, [("A", s)], emit, after=("B", s, 0) if a else ("B", s - 1, 1))
+            task(("B", s, a), {"S": 227 + CACC}, [("A", s)], emit, after=("B", s, 0) if a else ("B", s - 1, 1))
 
         def t_norm(m):
             def emit_max(e):
@@ -332,7 +334,7 @@ def tile_routingassignment_pa_t_w4_kernel(tc, x, adj_bytes, adj_scale, W_words, 
                     nc.scalar.activation(out=dst, in_=h[s][:, a, :], func=ACT.Relu, scale=f)
                 else:
                     nc.scalar.activation(out=dst, in_=h[s][:, a, :], func=ACT.Relu, scale=f, accum_out=acc)
-            engs = {"S": 231, "V": 124} if ph in BN else {"S": 250}
+            engs = {"S": 231, "V": 124} if ph in BN else {"S": 231 + CACC}
             task(("C", s, a), engs, [("n3", s // 2)], emit, after=("C", s, 0) if a else ("C", s - 1, 1))
 
         def t_sum_squares(ph, j, a):
@@ -344,7 +346,7 @@ def tile_routingassignment_pa_t_w4_kernel(tc, x, adj_bytes, adj_scale, W_words, 
                     junk2 = stream.tile([P, 2, K], F32, name="junk2", bufs=2)
                     nc.scalar.activation(out=junk2[:], in_=t, func=ACT.Square, accum_out=sq1[:, a, j : j + 1] if ph == 1 else sq2[ph][:, j : j + 1])
             deps = [("C", POS[1, g], a) for g in (2 * j, 2 * j + 1)] if ph == 1 else [("C", POS[ph, j], c) for c in (0, 1)]
-            task(("D", ph, j, a), {"V": 444} if ph in BN else {"S": 459}, deps, emit)
+            task(("D", ph, j, a), {"V": 444} if ph in BN else {"S": 440 + CACC}, deps, emit)
 
         coef = {}
 
@@ -384,7 +386,8 @@ def tile_routingassignment_pa_t_w4_kernel(tc, x, adj_bytes, adj_scale, W_words, 
             task(("f3", ph), {"V": 270}, [("f2", ph)], emit_coef)
 
         def t_affine(ph, q, i):
-            g4 = slice(4 * q, 4 * q + 4)
+            w = 2 if ph == 3 else 4
+            g4 = slice(w * q, w * q + w)
 
             def emit(e):
                 t = r1[:, g4, i, :] if ph == 1 else (r2 if ph == 2 else r3)[:, g4, :]
@@ -395,13 +398,12 @@ def tile_routingassignment_pa_t_w4_kernel(tc, x, adj_bytes, adj_scale, W_words, 
                     nc.vector.tensor_scalar(out=t, in0=t, scalar1=a, scalar2=c, op0=ALU.mult, op1=ALU.add)
                 else:
                     nc.gpsimd.tensor_scalar(out=t, in0=t, scalar1=a, scalar2=c, op0=ALU.mult, op1=ALU.add)
-            engs = {"V": 446, "S": 875}
-            if EG:
-                engs["G"] = 1150
+            engs = {"V": 231, "S": 450} if ph == 3 else {"V": 446, "S": 875}
             task(("E", ph, q, i), engs, [("f3", ph)], emit, prio=(EPRIO + 8 * ph + 2 * q + i) if ph < 3 else None)
 
         def t_store(ph, q):
-            g4 = slice(4 * q, 4 * q + 4)
+            w = 2 if ph == 3 else 4
+            g4 = slice(w * q, w * q + w)
 
             def emit(e):
                 if ph == 1:
@@ -409,7 +411,7 @@ def tile_routingassignment_pa_t_w4_kernel(tc, x, adj_bytes, adj_scale, W_words, 
                 else:
                     n0 = 256 if ph == 2 else 384
                     nc.sync.dma_start(out=out[g4, n0 : n0 + P, :].rearrange("g p c -> p g c"), in_=(r2 if ph == 2 else r3)[:, g4, :])
-            task(("st", ph, q), {"D": 1900 if ph == 1 else 950}, [("E", ph, q, i) for i in range(2 if ph == 1 else 1)], emit)
+            task(("st", ph, q), {"D": 1900 if ph == 1 else 950 if ph == 2 else 500}, [("E", ph, q, i) for i in range(2 if ph == 1 else 1)], emit)
 
         def emit_scale(e):
             psc = psum.tile([P, 4, P], F32, name="psA", bufs=4)
@@ -426,25 +428,24 @@ def tile_routingassignment_pa_t_w4_kernel(tc, x, adj_bytes, adj_scale, W_words, 
 
         task(("scale0", 0), {"D": 2600}, [], lambda e: None)
         tasks.pop(("scale0", 0))
-        tasks[("boot", 0)] = {"engs": {"S": 4760}, "deps": {}, "emit": lambda e: None, "prio": -1}
+        tasks[("boot", 0)] = {"engs": {"S": 4200}, "deps": {}, "emit": lambda e: None, "prio": -1}
         task(("scale1", 0), {"T": 760}, [("boot", 0)], lambda e: None)
         task(("scale", 0), {"S": 880}, [("scale1", 0)], emit_scale)
         task(("bias", 0), {"S": 440}, [("scale", 0)], emit_bias)
 
         load_x(0)
-        if LORD:
-            load_x(1)
-            load_adj1(0, 0, 2)
-        else:
-            load_adj1(0, 0, 2)
-            load_x(1)
+        load_x(1)
+        load_adj1(0, 0, 2)
+        load_adj23(2, 0, 1)
         load_x(2)
-        load_adj1(1, 2, 4)
         task(("lw", 0), {"D": 600}, [], load_w, after=last_load[0])
         load_x(3)
-        load_adj1(2, 4, 8)
+        load_adj1(1, 2, 4)
+        load_adj23(2, 1, 2)
         load_x(4)
         load_x(5)
+        load_adj1(2, 4, 6)
+        load_adj23(2, 2, 3)
         done_x = 0
         next_load = [6]
 
@@ -455,12 +456,13 @@ def tile_routingassignment_pa_t_w4_kernel(tc, x, adj_bytes, adj_scale, W_words, 
             if next_load[0] < G:
                 load_x(next_load[0])
                 next_load[0] += 1
-                if next_load[0] == 9:
-                    load_adj1(3, 8, 16)
-                if next_load[0] == (7 if MIX else 13):
-                    load_adj23(2)
-                if next_load[0] == 15:
-                    load_adj23(3)
+                if next_load[0] % 2 == 0:
+                    j = next_load[0] // 2 - 1
+                    load_adj1(j, 2 * j, 2 * j + 2)
+                    load_adj23(2, j, j + 1)
+                if next_load[0] == G:
+                    load_adj23(3, 0, 4)
+                    load_adj23(3, 4, 8)
 
         for k in range(-1, STEPS + 8):
             if k >= 0:
@@ -493,7 +495,7 @@ def tile_routingassignment_pa_t_w4_kernel(tc, x, adj_bytes, adj_scale, W_words, 
                 for ph, last in ((1, (1, 15)), (2, (2, 7)), (3, (3, 7))):
                     if k - 6 == POS[last]:
                         t_finish(ph)
-                        for q in range(4):
+                        for q in range(8 if ph == 3 else 4):
                             for i in range(2 if ph == 1 else 1):
                                 t_affine(ph, q, i)
                             t_store(ph, q)

from contextlib import ExitStack

import concourse.mybir as mybir
from concourse.masks import make_identity

G, N, F, K = 16, 512, 512, 256
P = 128
FLOPS = 2 * G * N * N * F + 2 * G * N * F * K
BN_EPS = 1e-5
NORM_EPS = 1e-12

F32 = mybir.dt.float32
BF16 = mybir.dt.bfloat16
U32 = mybir.dt.uint32
I32 = mybir.dt.int32
U8 = mybir.dt.uint8
FP8 = mybir.dt.float8_e4m3fn
FP8X4 = mybir.dt.float8_e4m3fn_x4
FP4X4 = mybir.dt.float4_e2m1fn_x4
ACT = mybir.ActivationFunctionType
ALU = mybir.AluOpType
AXX = mybir.AxisListType.X

BN = (2, 3)
XPARTS = 4
XS = 1
PRIO = "text"
XBUF = 6
LEAD = 1
HB = 6
SB = 4
EG = 0
EPRIO = 100000
CXS = 3000
CXV = 1126
CT = 1000
CACC = 50

ORDER = [step for j in range(8) for step in ((1, 2 * j), (1, 2 * j + 1)) + (((2, j - 1),) if j > 0 else ())] + [(2, 7)] + [(3, j) for j in range(8)]
STEPS = len(ORDER)
POS = {kind: i for i, kind in enumerate(ORDER)}
LAT = {"V": 160, "S": 120, "T": 150, "G": 150, "D": 2000}


def list_schedule(tasks):
    names = list(tasks)
    rank = {n: tasks[n]["prio"] for n in names}
    users = {n: [] for n in names}
    waits = {}
    for n in names:
        waits[n] = len(tasks[n]["deps"])
        for d in tasks[n]["deps"]:
            users[d].append(n)
    ready = {n: 0.0 for n in names if waits[n] == 0}
    at = {n: 0.0 for n in names}
    free = {e: 0.0 for e in "VSTGD"}
    last_pe = ""
    order = []
    end = 0.0
    while ready:
        best = None
        for n in ready:
            t = tasks[n]
            opt = min((max(free[e], at[n]) + c, e) for e, c in t["engs"].items())
            start = max(free[opt[1]], at[n])
            key = (start, rank[n])
            if best is None or key < best[0]:
                best = (key, n, opt[1])
        (start, r), n, e = best
        c = tasks[n]["engs"][e]
        if e == "T":
            if last_pe and last_pe != n[0][0]:
                c += 90
            last_pe = n[0][0]
        free[e] = start + c
        done = start + c + LAT[e]
        end = max(end, done)
        order.append((start, n, e))
        ready.pop(n)
        for u in users[n]:
            at[u] = max(at[u], start if tasks[u]["deps"][n] == "order" else done)
            waits[u] -= 1
            if waits[u] == 0:
                ready[u] = at[u]
    assert len(order) == len(names), [n for n in names if waits[n] > 0][:10]
    return order


def tile_routingassignment_pa_t_w4_kernel(tc, x, adj_bytes, adj_scale, W_words, W_scales, b, out):
    nc = tc.nc
    tasks = {}

    def task(name, engs, deps, emit, prio=None, after=None):
        d = {n: "data" for n in deps if n in tasks}
        if after is not None and after in tasks and after not in d:
            d[after] = "order"
        tasks[name] = {"engs": engs, "deps": d, "emit": emit, "prio": prio if prio is not None else len(tasks)}

    with ExitStack() as ctx:
        keep = ctx.enter_context(tc.tile_pool(name="keep", bufs=1))
        stream = ctx.enter_context(tc.tile_pool(name="stream", bufs=3))
        psum = ctx.enter_context(tc.psum_pool(name="psum", bufs=2))

        warm = keep.tile([P, 1], F32, name="warm")
        warm2 = keep.tile([P, 1], F32, name="warm2")
        nc.vector.memset(warm[:], 1.0)
        nc.scalar.activation(out=warm2[:], in_=warm[:], func=ACT.Sqrt)
        scale_col = keep.tile([P, 4], F32, name="scale_col")
        with nc.allow_non_contiguous_dma(reason="one scale to a partition"):
            nc.scalar.dma_start(out=scale_col[:], in_=adj_scale.rearrange("a b (m q) -> q (a b m)", q=P))
        w_sb = keep.tile([P, 2 * K], U8, name="w_sb", align_bytes=64)
        w_sc = keep.tile([P, K], U8, name="w_sc", align_bytes=64)
        b_row = keep.tile([P, K], BF16, name="b_row")
        ones = keep.tile([P, P], BF16, name="ones")
        ident = keep.tile([P, P], F32, name="ident")
        make_identity(nc, ident[:])
        nc.gpsimd.memset(w_sc[:].bitcast(U32), 0)
        nc.gpsimd.memset(b_row[:], 0.0)
        nc.gpsimd.memset(ones[:], 1.0)
        nc.scalar.dma_start(out=b_row[0:1, :], in_=b.rearrange("(o c) -> o c", o=1))

        scale2 = keep.tile([P, 2, N], F32, name="scale2")
        bias2 = keep.tile([P, 2, K], F32, name="bias2")
        xc = [keep.tile([P, F], U32, name="xc%d" % g, align_bytes=64) for g in range(G)]
        xs = [keep.tile([P, F], U8, name="xs%d" % g, align_bytes=64) for g in range(G)]
        r1 = keep.tile([P, G, 2, K], F32, name="r1")
        r2 = keep.tile([P, G, K], F32, name="r2")
        r3 = keep.tile([P, G, K], F32, name="r3")
        sum1 = keep.tile([P, G, 2], F32, name="sum1")
        sq1 = keep.tile([P, 2, 8], F32, name="sq1")
        sum2 = {2: keep.tile([P, G], F32, name="sum2_2"), 3: keep.tile([P, G], F32, name="sum2_3")}
        sq2 = {2: keep.tile([P, 8], F32, name="sq2_2"), 3: keep.tile([P, 8], F32, name="sq2_3")}
        bst = {2: keep.tile([P, 8, 6], F32, name="bst2"), 3: keep.tile([P, 8, 6], F32, name="bst3")}
        adj2 = keep.tile([P, G, N], U8, name="adj2")
        adj3 = keep.tile([P, G, N], U8, name="adj3")
        adj1 = {}

        x_raw, x_grp, sc, psT, ag, ac, asc, psA, gg, gc, gsc, psH, h, ss, ssm, nrm, rinv = ({} for _ in range(17))

        def graphs(s):
            ph, i = ORDER[s]
            return (i, i) if ph == 1 else (2 * i, 2 * i + 1)

        def load_x(g):
            def emit(e):
                x_raw[g] = stream.tile([P, 4, F], BF16, name="x_raw", bufs=XBUF)
                if g == 0:
                    for hf in range(2):
                        cols = slice(hf * F // 2, (hf + 1) * F // 2)
                        nc.sync.dma_start(out=x_raw[g][:, :, cols], in_=x[g].rearrange("(p t) f -> p t f", t=4)[:, :, cols])
                else:
                    nc.sync.dma_start(out=x_raw[g][:], in_=x[g].rearrange("(p t) f -> p t f", t=4))
            task(("lx", g), {"D": 940}, [("xg", g - XBUF, i) for i in range(XPARTS)], emit, after=last_load[0])
            last_load[0] = ("lx", g)

        def load_adj1(c, g0, g1):
            def emit(e):
                t = keep.tile([P, g1 - g0, 2 * N], U8, name="adj1_%d" % c)
                nc.sync.dma_start(out=t[:], in_=adj_bytes[g0:g1, 0:256, :].rearrange("g (p r) j -> p g (r j)", r=2))
                for g in range(g0, g1):
                    adj1[g] = (t, g - g0)
            task(("la", c), {"D": 250 * (g1 - g0)}, [], emit, after=last_load[0])
            last_load[0] = ("la", c)
            for g in range(g0, g1):
                la_of[1, g] = ("la", c)

        def load_adj23(ph, j0, j1):
            t, n0 = (adj2, 256) if ph == 2 else (adj3, 384)
            gs = slice(2 * j0, 2 * j1)

            def emit(e):
                nc.sync.dma_start(out=t[:, gs, :], in_=adj_bytes[gs, n0 : n0 + P, :].rearrange("g p j -> p g j"))
            task(("lb", ph, j0), {"D": 400 * (j1 - j0)}, [], emit, after=last_load[0])
            last_load[0] = ("lb", ph, j0)
            for j in range(j0, j1):
                la_of[ph, j] = ("lb", ph, j0)

        la_of = {}
        last_load = [None]

        def load_w(e):
            nc.sync.dma_start(out=w_sb[:], in_=W_words[0])
            for q in range(4):
                nc.sync.dma_start(out=w_sc[32 * q : 32 * q + 4, :].bitcast(I32), in_=W_scales[0, 4 * q : 4 * q + 4, :].bitcast(I32))

        def t_x_group(g, i):
            m = slice(i * P // XPARTS, (i + 1) * P // XPARTS)

            def emit(e):
                if i == 0:
                    x_grp[g] = stream.tile([P, 4, P, 4], BF16, name="x_grp", bufs=3, align_bytes=64)
                o = x_grp[g][:].rearrange("p c m t -> p m c t")[:, m]
                n = x_raw[g][:].rearrange("p t (m c) -> p m c t", c=4)[:, m]
                if e == "V":
                    nc.vector.tensor_copy(out=o, in_=n)
                else:
                    nc.scalar.copy(out=o, in_=n)
            engs = {"V": 16 + CXV / XPARTS}
            if XS:
                engs["S"] = 12 + CXS / XPARTS
            task(("xg", g, i), engs, [("lx", g), ("xq", g - 3)], emit, after=("xg", g - 1, XPARTS - 1) if i == 0 else ("xg", g, i - 1))

        def t_x_quant(g):
            def emit(e):
                nc.vector.quantize_mx(out=xc[g][:].bitcast(FP8X4), scales=xs[g][:], in_=x_grp[g][:].rearrange("p c m t -> p (c m t)"))
            task(("xq", g), {"V": 467}, [("xg", g, i) for i in range(XPARTS)], emit)

        def t_scale(s):
            def emit(e):
                sc[s] = stream.tile([P, 2 * N], BF16, name="sc", bufs=SB, align_bytes=64)
                g0, g1 = graphs(s)
                if ORDER[s][0] == 1:
                    t, i = adj1[g0]
                    src = t[:, i, :]
                else:
                    src = (adj2 if ORDER[s][0] == 2 else adj3)[:, g0 : g1 + 1, :].rearrange("p g j -> p (g j)")
                nc.vector.tensor_tensor(out=sc[s][:], in0=src.bitcast(FP8), in1=scale2[:].rearrange("p a j -> p (a j)"), op=ALU.mult)
            task(("sc", s), {"V": 872}, [la_of[ORDER[s]], ("scale", 0), ("T", s - SB)], emit, after=("sc", s - 1))

        def t_transpose(s):
            def emit(e):
                psT[s] = psum.tile([P, 2, 2, P], F32, name="psT", bufs=2)
                words = sc[s][:].bitcast(F32)
                for a in range(2):
                    for u in range(2):
                        nc.tensor.transpose(psT[s][:, a, u, :], words[:, 256 * a + u : 256 * (a + 1) : 2], ident[:])
            task(("T", s), {"T": CT}, [("sc", s), ("te", s - 2)], emit, after=("T", s - 1))

        def copy(e, o, n):
            if e == "V":
                nc.vector.tensor_copy(out=o, in_=n)
            else:
                nc.scalar.copy(out=o, in_=n)

        def t_adj_exit(s):
            def emit(e):
                ag[s] = stream.tile([P, 8 * P], BF16, name="ag", bufs=SB, align_bytes=64)
                copy(e, ag[s][:].bitcast(F32).rearrange("p (a n u) -> p a n u", a=2, u=2), psT[s][:].rearrange("p a u n -> p a n u"))
            engs = {"S": 440}
            task(("te", s), engs, [("T", s), ("q", s - SB)], emit, after=("te", s - 1))

        def t_adj_quant(s):
            def emit(e):
                ac[s] = stream.tile([P, 2 * P], U32, name="ac", bufs=SB, align_bytes=64)
                asc[s] = stream.tile([P, 2 * P], U8, name="asc", bufs=SB, align_bytes=64)
                nc.vector.quantize_mx(out=ac[s][:].bitcast(FP8X4), scales=asc[s][:], in_=ag[s][:])
            task(("q", s), {"V": 241}, [("te", s), ("M", s - SB, 1)], emit, after=("q", s - 1))

        def t_agg(s, a):
            def emit(e):
                g = graphs(s)[a]
                psA[s, a] = psum.tile([P, 4, P], F32, name="psA", bufs=4)
                rows = slice(P * a, P * (a + 1))
                for t in range(4):
                    cols = slice(P * t, P * (t + 1))
                    nc.tensor.matmul_mx(
                        out=psA[s, a][:, t, :],
                        lhsT=xc[g][:, cols].bitcast(FP8X4), lhsT_scale=xs[g][:, cols],
                        rhs=ac[s][:, rows].bitcast(FP8X4), rhs_scale=asc[s][:, rows],
                        start=True, stop=True)
            task(("M", s, a), {"T": 455}, [("q", s), ("xq", graphs(s)[a]), ("ae", s - 2, a)], emit, after=("M", s, 0) if a else ("M", s - 1, 1))

        def t_agg_exit(s, a):
            def emit(e):
                if a == 0:
                    gg[s] = stream.tile([P, 2, P, 4], BF16, name="gg", bufs=SB, align_bytes=64)
                copy(e, gg[s][:, a], psA[s, a][:].rearrange("p t n -> p n t"))
            engs = {"S": 440}
            task(("ae", s, a), engs, [("M", s, a), ("qa", s - SB)], emit, after=("ae", s, 0) if a else ("ae", s - 1, 1))

        def t_agg_quant(s):
            def emit(e):
                gc[s] = stream.tile([P, 2 * P], U32, name="gc", bufs=SB, align_bytes=64)
                gsc[s] = stream.tile([P, 2 * P], U8, name="gsc", bufs=SB, align_bytes=64)
                nc.vector.quantize_mx(out=gc[s][:].bitcast(FP8X4), scales=gsc[s][:], in_=gg[s][:].rearrange("p a n t -> p (a n t)"))
            task(("qa", s), {"V": 241}, [("ae", s, 0), ("ae", s, 1), ("H", s - SB)], emit, after=("qa", s - 1))

        def t_h(s):
            def emit(e):
                psH[s] = psum.tile([P, 2, K], F32, name="psH", bufs=2)
                for a in range(2):
                    rows = slice(P * a, P * (a + 1))
                    nc.tensor.matmul_mx(
                        out=psH[s][:, a, :],
                        lhsT=gc[s][:, rows].bitcast(FP8X4), lhsT_scale=gsc[s][:, rows],
                        rhs=w_sb[:].bitcast(FP4X4), rhs_scale=w_sc[:],
                        start=True, stop=True)
            task(("H", s), {"T": 445}, [("qa", s), ("lw", 0), ("A", s - 2)], emit, after=("H", s - 1))

        def t_bias(s):
            def emit(e):
                h[s] = stream.tile([P, 2, K], F32, name="h", bufs=HB)
                nc.vector.tensor_tensor(out=h[s][:], in0=psH[s][:], in1=bias2[:], op=ALU.add)
            task(("A", s), {"V": 444}, [("H", s), ("bias", 0), ("C", s - HB, 0), ("C", s - HB, 1)], emit, after=("A", s - 1))

        def t_square(s, a):
            def emit(e):
                if s % 2 == 0 and a == 0:
                    ss[s // 2] = stream.tile([P, 4], F32, name="ss")
                junk = stream.tile([P, K], F32, name="junk", bufs=2)
                col = 2 * (s % 2) + a
                nc.scalar.activation(out=junk[:], in_=h[s][:, a, :], func=ACT.Square, accum_out=ss[s // 2][:, col : col + 1])
            task(("B", s, a), {"S": 227 + CACC}, [("A", s)], emit, after=("B", s, 0) if a else ("B", s - 1, 1))

        def t_norm(m):
            def emit_max(e):
                ssm[m] = stream.tile([P, 4], F32, name="ssm")
                nc.gpsimd.tensor_scalar(out=ssm[m][:], in0=ss[m][:], scalar1=NORM_EPS * NORM_EPS, scalar2=None, op0=ALU.max)

            def emit_sqrt(e):
                nrm[m] = stream.tile([P, 4], F32, name="nrm")
                nc.scalar.activation(out=nrm[m][:], in_=ssm[m][:], func=ACT.Sqrt)

            def emit_recip(e):
                rinv[m] = stream.tile([P, 4], F32, name="rinv")
                nc.vector.reciprocal(out=rinv[m][:], in_=nrm[m][:])
            task(("n1", m), {"G": 125}, [("B", s, a) for s in (2 * m, 2 * m + 1) for a in (0, 1)], emit_max, after=("n1", m - 1))
            task(("n2", m), {"S": 45}, [("n1", m)], emit_sqrt, after=("n2", m - 1))
            task(("n3", m), {"V": 55}, [("n2", m)], emit_recip, after=("n3", m - 1))

        def t_relu(s, a):
            ph, i = ORDER[s]

            def emit(e):
                g0, g1 = graphs(s)
                f = rinv[s // 2][:, 2 * (s % 2) + a : 2 * (s % 2) + a + 1]
                if ph == 1:
                    dst, acc = r1[:, g0, a, :], sum1[:, g0, a : a + 1]
                else:
                    dst, acc = (r2 if ph == 2 else r3)[:, g0 + a, :], sum2[ph][:, g0 + a : g0 + a + 1]
                if e == "V":
                    nc.vector.tensor_scalar(out=dst, in0=h[s][:, a, :], scalar1=f, scalar2=0.0, op0=ALU.mult, op1=ALU.max)
                elif ph in BN:
                    nc.scalar.activation(out=dst, in_=h[s][:, a, :], func=ACT.Relu, scale=f)
                else:
                    nc.scalar.activation(out=dst, in_=h[s][:, a, :], func=ACT.Relu, scale=f, accum_out=acc)
            engs = {"S": 231, "V": 124} if ph in BN else {"S": 231 + CACC}
            task(("C", s, a), engs, [("n3", s // 2)], emit, after=("C", s, 0) if a else ("C", s - 1, 1))

        def t_sum_squares(ph, j, a):
            def emit(e):
                t = r1[:, 2 * j : 2 * j + 2, a, :] if ph == 1 else (r2 if ph == 2 else r3)[:, 2 * j : 2 * j + 2, :]
                if ph in BN:
                    nc.vector.bn_stats(out=bst[ph][:, j, :], in_=t.rearrange("p g c -> p (g c)"))
                else:
                    junk2 = stream.tile([P, 2, K], F32, name="junk2", bufs=2)
                    nc.scalar.activation(out=junk2[:], in_=t, func=ACT.Square, accum_out=sq1[:, a, j : j + 1] if ph == 1 else sq2[ph][:, j : j + 1])
            deps = [("C", POS[1, g], a) for g in (2 * j, 2 * j + 1)] if ph == 1 else [("C", POS[ph, j], c) for c in (0, 1)]
            task(("D", ph, j, a), {"V": 444} if ph in BN else {"S": 440 + CACC}, deps, emit)

        coef = {}

        def t_finish(ph):
            n = 2 if ph == 1 else 1
            st = {}

            def emit_var(e):
                varp = keep.tile([P, n], F32, name="varp%d" % ph)
                if ph not in BN:
                    mean = keep.tile([P, n], F32, name="mean%d" % ph)
                    e2 = keep.tile([P, n], F32, name="e2_%d" % ph)
                    m2 = keep.tile([P, n], F32, name="m2_%d" % ph)
                    nc.vector.tensor_reduce(out=mean[:], in_=sum1[:].rearrange("p g a -> p a g") if ph == 1 else sum2[ph][:], axis=AXX, op=ALU.add)
                    nc.vector.tensor_reduce(out=e2[:], in_=sq1[:] if ph == 1 else sq2[ph][:], axis=AXX, op=ALU.add)
                    nc.vector.tensor_scalar(out=mean[:], in0=mean[:], scalar1=1.0 / (G * K), scalar2=None, op0=ALU.mult)
                    nc.vector.tensor_tensor(out=m2[:], in0=mean[:], in1=mean[:], op=ALU.mult)
                    nc.vector.scalar_tensor_tensor(out=varp[:], in0=e2[:], scalar=1.0 / (G * K), in1=m2[:], op0=ALU.mult, op1=ALU.subtract)
                    nc.vector.tensor_scalar(out=varp[:], in0=varp[:], scalar1=BN_EPS, scalar2=None, op0=ALU.add)
                else:
                    mean = keep.tile([P, 2], F32, name="mv%d" % ph)
                    nc.vector.bn_aggr(out=mean[:], in_=bst[ph][:].rearrange("p i s -> p (i s)"))
                    nc.vector.tensor_scalar(out=varp[:], in0=mean[:, 1:2], scalar1=BN_EPS, scalar2=None, op0=ALU.add)
                st["mean"], st["varp"] = mean, varp

            def emit_sqrt(e):
                st["root"] = keep.tile([P, n], F32, name="root%d" % ph)
                nc.scalar.activation(out=st["root"][:], in_=st["varp"][:], func=ACT.Sqrt)

            def emit_coef(e):
                cf = keep.tile([P, n, 2], F32, name="coef%d" % ph)
                nc.vector.reciprocal(out=cf[:, :, 0], in_=st["root"][:])
                nc.vector.scalar_tensor_tensor(out=cf[:, :, 1], in0=st["mean"][:, 0:n], scalar=-1.0, in1=cf[:, :, 0], op0=ALU.mult, op1=ALU.mult)
                coef[ph] = cf
            task(("f1", ph), {"V": 420 if ph in BN else 900}, [("D", ph, j, a) for j in range(8) for a in range(n)], emit_var)
            task(("f2", ph), {"S": 45}, [("f1", ph)], emit_sqrt)
            task(("f3", ph), {"V": 270}, [("f2", ph)], emit_coef)

        def t_affine(ph, q, i):
            w = 2 if ph == 3 else 4
            g4 = slice(w * q, w * q + w)

            def emit(e):
                t = r1[:, g4, i, :] if ph == 1 else (r2 if ph == 2 else r3)[:, g4, :]
                a, c = coef[ph][:, i, 0:1], coef[ph][:, i, 1:2]
                if e == "S":
                    nc.scalar.activation(out=t, in_=t, func=ACT.Identity, scale=a, bias=c)
                elif e == "V":
                    nc.vector.tensor_scalar(out=t, in0=t, scalar1=a, scalar2=c, op0=ALU.mult, op1=ALU.add)
                else:
                    nc.gpsimd.tensor_scalar(out=t, in0=t, scalar1=a, scalar2=c, op0=ALU.mult, op1=ALU.add)
            engs = {"V": 231, "S": 450} if ph == 3 else {"V": 446, "S": 875}
            task(("E", ph, q, i), engs, [("f3", ph)], emit, prio=(EPRIO + 8 * ph + 2 * q + i) if ph < 3 else None)

        def t_store(ph, q):
            w = 2 if ph == 3 else 4
            g4 = slice(w * q, w * q + w)

            def emit(e):
                if ph == 1:
                    nc.sync.dma_start(out=out[g4, 0:256, :].rearrange("g (p r) c -> p g (r c)", r=2), in_=r1[:, g4].rearrange("p g r c -> p g (r c)"))
                else:
                    n0 = 256 if ph == 2 else 384
                    nc.sync.dma_start(out=out[g4, n0 : n0 + P, :].rearrange("g p c -> p g c"), in_=(r2 if ph == 2 else r3)[:, g4, :])
            task(("st", ph, q), {"D": 1900 if ph == 1 else 950 if ph == 2 else 500}, [("E", ph, q, i) for i in range(2 if ph == 1 else 1)], emit)

        def emit_scale(e):
            psc = psum.tile([P, 4, P], F32, name="psA", bufs=4)
            for m in range(4):
                nc.tensor.transpose(psc[:, m, :], scale_col[:, m : m + 1].to_broadcast([P, P]), ident[:])
            nc.scalar.copy(out=scale2[:, 0, :], in_=psc[:].rearrange("p m q -> p (m q)"))
            nc.scalar.copy(out=scale2[:, 1, :], in_=psc[:].rearrange("p m q -> p (m q)"))

        def emit_bias(e):
            psb = psum.tile([P, 2, K], F32, name="psH", bufs=2)
            for a in range(2):
                nc.tensor.matmul(psb[:, a, :], lhsT=ones[:], rhs=b_row[:], start=True, stop=True)
            nc.scalar.copy(out=bias2[:], in_=psb[:])

        task(("scale0", 0), {"D": 2600}, [], lambda e: None)
        tasks.pop(("scale0", 0))
        tasks[("boot", 0)] = {"engs": {"S": 4200}, "deps": {}, "emit": lambda e: None, "prio": -1}
        task(("scale1", 0), {"T": 760}, [("boot", 0)], lambda e: None)
        task(("scale", 0), {"S": 880}, [("scale1", 0)], emit_scale)
        task(("bias", 0), {"S": 440}, [("scale", 0)], emit_bias)

        load_x(0)
        load_x(1)
        load_adj1(0, 0, 2)
        load_adj23(2, 0, 1)
        load_x(2)
        task(("lw", 0), {"D": 600}, [], load_w, after=last_load[0])
        load_x(3)
        load_adj1(1, 2, 4)
        load_adj23(2, 1, 2)
        load_x(4)
        load_x(5)
        load_adj1(2, 4, 6)
        load_adj23(2, 2, 3)
        done_x = 0
        next_load = [6]

        def do_x(g):
            for i in range(XPARTS):
                t_x_group(g, i)
            t_x_quant(g)
            if next_load[0] < G:
                load_x(next_load[0])
                next_load[0] += 1
                if next_load[0] % 2 == 0:
                    j = next_load[0] // 2 - 1
                    load_adj1(j, 2 * j, 2 * j + 2)
                    load_adj23(2, j, j + 1)
                if next_load[0] == G:
                    load_adj23(3, 0, 4)
                    load_adj23(3, 4, 8)

        for k in range(-1, STEPS + 8):
            if k >= 0:
                if k < STEPS:
                    t_transpose(k)
                    t_adj_exit(k)
                if 0 <= k - 1 < STEPS:
                    t_adj_quant(k - 1)
                    for a in range(2):
                        t_agg(k - 1, a)
                        t_agg_exit(k - 1, a)
                if 0 <= k - 2 < STEPS:
                    t_agg_quant(k - 2)
                    t_h(k - 2)
                    t_bias(k - 2)
                if 0 <= k - 3 < STEPS:
                    for a in range(2):
                        t_square(k - 3, a)
                    if (k - 3) % 2 == 1:
                        t_norm((k - 3) // 2)
                if 0 <= k - 5 < STEPS:
                    for a in range(2):
                        t_relu(k - 5, a)
                    ph, i = ORDER[k - 5]
                    if ph > 1:
                        t_sum_squares(ph, i, 0)
                    elif i % 2 == 1:
                        t_sum_squares(1, i // 2, 0)
                        t_sum_squares(1, i // 2, 1)
                for ph, last in ((1, (1, 15)), (2, (2, 7)), (3, (3, 7))):
                    if k - 6 == POS[last]:
                        t_finish(ph)
                        for q in range(8 if ph == 3 else 4):
                            for i in range(2 if ph == 1 else 1):
                                t_affine(ph, q, i)
                            t_store(ph, q)
            while done_x < G and k + LEAD >= POS[1, done_x]:
                do_x(done_x)
                done_x += 1
            if k + 1 < STEPS:
                t_scale(k + 1)

        if PRIO == "bottom":
            names = list(tasks)
            users = {n: [] for n in names}
            for n in names:
                for d in tasks[n]["deps"]:
                    users[d].append(n)
            level = {}
            for n in reversed(names):
                t = tasks[n]
                level[n] = min(t["engs"].values()) + max([level[u] + 150 for u in users[n]] + [0])
            for n in names:
                tasks[n]["prio"] = -level[n]
        order = list_schedule(tasks)
        with tc.manual_schedule():
            for start, n, e in sorted(order, key=lambda r: r[0]):
                tasks[n]["emit"](e)
